import numpy as np
import ml_dtypes


def mxq(x, axis, fmt="e4m3"):
    dtype, down = {"e4m3": (ml_dtypes.float8_e4m3fn, 7), "e5m2": (ml_dtypes.float8_e5m2, 14)}[fmt]
    v = np.moveaxis(np.asarray(x, np.float32).astype(ml_dtypes.bfloat16).astype(np.float64), axis, -1)
    blocks = v.reshape(v.shape[:-1] + (-1, 32))
    amax = np.abs(blocks).max(-1, keepdims=True)
    byte = np.maximum(np.where(amax > 0, np.frexp(amax)[1] - 1 + 127, 0) - down, 1)
    scale = np.exp2(byte - 127.0)
    codes = (blocks / scale).astype(np.float32).astype(dtype).astype(np.float64)
    return np.moveaxis((codes * scale).reshape(v.shape), -1, axis)


WIDE = False


def mx_kscale(k):
    if not WIDE:
        return np.ones(k)
    levels = np.array([10, -10, 5, -5, 0])
    a = np.random.permutation(np.resize(levels, k // 512 * 4)).reshape(k // 512, 4)
    idx = np.arange(k)
    return np.exp2(a[idx // 512, idx % 128 // 32])


BF16 = ml_dtypes.bfloat16


def bf(x):
    return np.asarray(x, np.float32).astype(BF16)


def f64(x):
    return np.asarray(x).astype(np.float64)


E, T, G, C = 1536, 3, 3, 512
EPS = 1e-5


def silu(v):
    return v / (1.0 + np.exp(-v))


def sigmoid(v):
    return 1.0 / (1.0 + np.exp(-v))


def softplus(v):
    return np.maximum(v, 0.0) + np.log(1.0 + np.exp(-np.abs(v)))


def layer_norm(v, g, b):
    m = v.mean(-1, keepdims=True)
    var = ((v - m) ** 2).mean(-1, keepdims=True)
    return (v - m) / np.sqrt(var + EPS) * g + b


def setup_inputs():
    n = np.random.standard_normal
    s = mx_kscale(C)
    t = mx_kscale(C)
    r = np.sqrt(C)
    return {
        "edge": bf(n((E, C))),
        "h_k": bf(silu(n((E, T, C))) * s),
        "h_m": bf(silu(n((E, T, C))) * s),
        "Wq": bf(n((C, C)) * 0.3 / r),
        "bq": bf(0.2 + n(C) * 0.1),
        "Wk2": bf(n((C, C)) * 0.5 / r / s[:, None]),
        "bk2": bf(0.2 + n(C) * 0.1),
        "Wm2": bf(n((C, C)) * 1.5 / r / s[:, None] * t),
        "bm2": bf(n(C) * 0.2 * t),
        "Wc": bf(n((C, C)) / r / t[:, None]),
        "bc": bf(0.1 + n(C) * 0.1),
        "g_att": bf(1.0 + n(C) * 0.2),
        "b_att": bf(n(C) * 0.2),
        "g_bn": bf(1.0 + n(C) * 0.2),
        "b_bn": bf(n(C) * 0.2),
    }


def reference(edge, h_k, h_m, Wq, bq, Wk2, bk2, Wm2, bm2, Wc, bc, g_att, b_att, g_bn, b_bn):
    x = f64(edge)
    q = (mxq(x, 1, "e4m3") @ mxq(f64(Wq), 0, "e4m3")) + f64(bq)
    k = (mxq(f64(h_k), 2, "e4m3") @ mxq(f64(Wk2), 0, "e4m3")) + f64(bk2)
    msg = (mxq(f64(h_m), 2, "e4m3") @ mxq(f64(Wm2), 0, "e4m3")) + f64(bm2)
    alpha = q[:, None, :] * k / np.sqrt(C)
    gated = msg * sigmoid(layer_norm(alpha, f64(g_att), f64(b_att)))
    out = (mxq(gated, 2, "e4m3") @ mxq(f64(Wc), 0, "e4m3")) + f64(bc)
    out = out.sum(axis=1)
    return softplus(x + layer_norm(out, f64(g_bn), f64(b_bn)))

@@ -1,0 +1,399 @@
+import math
+from contextlib import ExitStack
+
+import concourse.mybir as mybir
+from concourse.masks import make_identity
+
+F32 = mybir.dt.float32
+BF16 = mybir.dt.bfloat16
+U32 = mybir.dt.uint32
+U8 = mybir.dt.uint8
+FP8X4 = mybir.dt.float8_e4m3fn_x4
+ALU = mybir.AluOpType
+ACT = mybir.ActivationFunctionType
+
+P = 128
+PACK = 4
+E, T, C = 1536, 3, 512
+GROUP = 512
+N_GROUPS = E // GROUP
+J = GROUP // P
+CT = C // P
+N_STEPS = N_GROUPS * T
+EPS = 1e-5
+STAT_BUFS = 2 * J
+
+LOAD_AHEAD = 3
+TRANSPOSE_AHEAD = 2
+QUANTISE_AHEAD = 1
+GATE_LAG = 1
+
+FLOPS = 2 * C * C * (E + 3 * E * T)
+
+
+def tile_comformerconvedgelayer_pb_t_kernel(
+    tc, edge, h_k, h_m, Wq, bq, Wk2, bk2, Wm2, bm2, Wc, bc, g_att, b_att, g_bn, b_bn, out
+):
+    nc = tc.nc
+    with ExitStack() as ctx:
+        sb = ctx.enter_context(tc.tile_pool(name="sb", bufs=1))
+        psum = ctx.enter_context(tc.psum_pool(name="psum", bufs=4))
+        ctx.enter_context(tc.manual_schedule())
+
+        def matmul_mx(acc, stationary, moving, start=True, stop=True):
+            nc.tensor.matmul_mx(
+                out=acc,
+                lhsT=stationary[0].bitcast(FP8X4),
+                lhsT_scale=stationary[1],
+                rhs=moving[0].bitcast(FP8X4),
+                rhs_scale=moving[1],
+                start=start,
+                stop=stop,
+            )
+
+        def columns(operand, i):
+            return operand[0][:, i * P : (i + 1) * P], operand[1][:, i * P : (i + 1) * P]
+
+        def whole(operand):
+            return operand[0][:], operand[1][:]
+
+        def quantise(grouped, width, tag, bufs):
+            codes = sb.tile([P, width], U32, tag=tag + "_codes", bufs=bufs, align_bytes=64)
+            scales = sb.tile([P, width], U8, tag=tag + "_scales", bufs=bufs, align_bytes=64)
+            nc.vector.quantize_mx(out=codes[:].bitcast(FP8X4), scales=scales[:], in_=grouped)
+            return codes, scales
+
+        def transposed_product(weight, moving):
+            banks = []
+            for ct in range(CT):
+                acc = psum.tile([P, GROUP], F32, tag="mx", name="acc")
+                matmul_mx(acc[:], columns(weight, ct), whole(moving))
+                banks.append(acc)
+            return banks
+
+        def small(tag):
+            return sb.tile([P, 1], F32, tag=tag, bufs=STAT_BUFS, name=tag)
+
+        def inverse_sqrt(x, tag):
+            y = small(tag)
+            nc.gpsimd.tensor_tensor(out=y[:], in0=x[:], in1=neg_half[:], op=ALU.pow)
+            return y
+
+        ident_f32 = sb.tile([P, P], F32)
+        make_identity(nc, ident_f32[:])
+        ident_bf16 = sb.tile([P, P], BF16)
+        make_identity(nc, ident_bf16[:])
+        neg_half = sb.tile([P, 1], F32)
+        nc.vector.memset(neg_half[:], -0.5)
+
+        vec_rows = sb.tile([P, P], BF16)
+        nc.vector.memset(vec_rows[:], 0.0)
+        for v, vec in enumerate((bq, bk2, bm2, g_att, b_att)):
+            nc.sync.dma_start(
+                out=vec_rows[v * CT : (v + 1) * CT, :], in_=vec.rearrange("(t p) -> t p", p=P)
+            )
+        cols_ps = psum.tile([P, P], BF16, tag="tp")
+        nc.tensor.transpose(cols_ps[:], vec_rows[:], ident_bf16[:])
+        cols = sb.tile([P, P], F32)
+        nc.vector.tensor_copy(out=cols[:], in_=cols_ps[:])
+        bk2_col = cols[:, 1 * CT : 2 * CT]
+        bm2_col = cols[:, 2 * CT : 3 * CT]
+        g_att_col = cols[:, 3 * CT : 4 * CT]
+        b_att_col = cols[:, 4 * CT : 5 * CT]
+        inv_sqrt_c = 1.0 / math.sqrt(C)
+        bq_scaled_col = sb.tile([P, CT], F32)
+        nc.vector.tensor_scalar_mul(out=bq_scaled_col[:], in0=cols[:, 0:CT], scalar1=inv_sqrt_c)
+
+        def load_weight(w_view, split):
+            raw = sb.tile([P, PACK, C], BF16, tag="w_raw", bufs=2)
+            nc.sync.dma_start(out=raw[:].rearrange(split, u=2), in_=w_view)
+            return raw
+
+        def load_first_stage_weight(w):
+            return load_weight(
+                w.rearrange("(u p e) c -> p u (e c)", u=2, p=P, e=2), "p (u e) c -> p u (e c)"
+            )
+
+        def load_second_stage_weight(w):
+            return load_weight(
+                w.rearrange("(u e p) c -> p u e c", u=2, e=2, p=P), "p (u e) c -> p u e c"
+            )
+
+        def quantise_weight(raw, name):
+            grouped = sb.tile([P, C, PACK], BF16, tag="w_grouped", align_bytes=64)
+            nc.vector.tensor_copy(out=grouped[:], in_=raw[:].rearrange("p t c -> p c t"))
+            return quantise(grouped[:].rearrange("p c t -> p (c t)"), C, name, 1)
+
+        edge_v = edge.rearrange("(g p j) c -> g p j c", g=N_GROUPS, p=P)
+        hk_v = h_k.rearrange("(g p j) t c -> g p j t c", g=N_GROUPS, p=P)
+        hm_v = h_m.rearrange("(g p j) t c -> g p j t c", g=N_GROUPS, p=P)
+        out_v = out.rearrange("(g p j) c -> g p j c", g=N_GROUPS, p=P)
+
+        edge_rows, edge_grouped, edge_q, q_t = {}, {}, {}, {}
+        hk_rows, hk_grouped, hk_q, k_banks = {}, {}, {}, {}
+        hm_rows, hm_grouped, hm_q, msg_banks = {}, {}, {}, {}
+        alpha_t, normed, gate_t, gated_q = {}, {}, {}, {}
+        v_rows, v_stats, residual, softplus = {}, {}, {}, {}
+
+        def load_rows(view, tag, bufs):
+            rows = sb.tile([P, J, C], BF16, tag=tag, bufs=bufs)
+            nc.sync.dma_start(out=rows[:], in_=view)
+            return rows
+
+        def is_step(s):
+            return 0 <= s < N_STEPS
+
+        def starts_group(s):
+            return is_step(s) and s % T == 0
+
+        def load_step(s):
+            if starts_group(s + 1):
+                edge_rows[(s + 1) // T] = load_rows(edge_v[(s + 1) // T], "edge_rows", N_GROUPS)
+            if is_step(s):
+                g, t = divmod(s, T)
+                hk_rows[s] = load_rows(hk_v[g][:, :, t, :], "hk_rows", LOAD_AHEAD)
+                hm_rows[s] = load_rows(hm_v[g][:, :, t, :], "hm_rows", LOAD_AHEAD)
+
+        def transpose_rows(rows):
+            grouped = sb.tile([P, PACK * GROUP], BF16, tag="x_grouped", bufs=3, align_bytes=64)
+            grouped_words = grouped[:].bitcast(F32).rearrange("p (n u) -> p n u", u=2)
+            for half in range(2):
+                bank = psum.tile([P, 2, 2 * P], F32, tag="tp")
+                for jj in range(2):
+                    words = rows[:, 2 * half + jj, :].bitcast(F32)
+                    for u in range(2):
+                        nc.tensor.transpose(
+                            bank[:, u, jj * P : (jj + 1) * P],
+                            words[:, u * P : (u + 1) * P],
+                            ident_f32[:],
+                        )
+                nc.scalar.copy(
+                    out=grouped_words[:, half * 2 * P : (half + 1) * 2 * P, :],
+                    in_=bank[:].rearrange("p u n -> p n u"),
+                )
+            return grouped
+
+        def transpose_step(s):
+            if starts_group(s + 1):
+                edge_grouped[(s + 1) // T] = transpose_rows(edge_rows[(s + 1) // T])
+            if is_step(s):
+                hk_grouped[s] = transpose_rows(hk_rows[s])
+                hm_grouped[s] = transpose_rows(hm_rows[s])
+
+        def quantise_step(s):
+            if starts_group(s + 1):
+                edge_q[(s + 1) // T] = quantise(edge_grouped[(s + 1) // T][:], GROUP, "edge", 2)
+            if is_step(s):
+                hk_q[s] = quantise(hk_grouped[s][:], GROUP, "hk", 2)
+                hm_q[s] = quantise(hm_grouped[s][:], GROUP, "hm", QUANTISE_AHEAD + GATE_LAG + 1)
+
+        def q_project(g):
+            banks = transposed_product(wq, edge_q[g])
+            q_t[g] = sb.tile([P, CT, GROUP], F32, tag="q_t", bufs=2, name="q_t")
+            for ct in range(CT):
+                nc.scalar.activation(
+                    out=q_t[g][:, ct, :], in_=banks[ct][:], func=ACT.Identity,
+                    bias=bq_scaled_col[:, ct : ct + 1], scale=inv_sqrt_c,
+                )
+
+        def k_project(s):
+            k_banks[s] = transposed_product(wk, hk_q[s])
+
+        def alpha(s):
+            alpha_t[s] = sb.tile([P, CT, GROUP], F32, tag="alpha_t", name="alpha_t")
+            for ct in range(CT):
+                nc.vector.scalar_tensor_tensor(
+                    out=alpha_t[s][:, ct, :], in0=k_banks[s][ct][:], scalar=bk2_col[:, ct : ct + 1],
+                    in1=q_t[s // T][:, ct, :], op0=ALU.add, op1=ALU.mult,
+                )
+
+        def normalise(s):
+            normed[s] = sb.tile([P, J, C], F32, tag="normed", bufs=2, name="normed")
+            for j in range(J):
+                bank = psum.tile([P, C], F32, tag="tp")
+                for ct in range(CT):
+                    nc.tensor.transpose(
+                        bank[:, ct * P : (ct + 1) * P],
+                        alpha_t[s][:, ct, j * P : (j + 1) * P],
+                        ident_f32[:],
+                    )
+                stats = sb.tile([P, 6], F32, tag="alpha_stats", bufs=STAT_BUFS)
+                nc.vector.bn_stats(out=stats[:], in_=bank[:])
+                mean_var = sb.tile([P, 2], F32, tag="alpha_mean_var", bufs=STAT_BUFS)
+                nc.vector.bn_aggr(out=mean_var[:], in_=stats[:])
+                var_eps = small("alpha_var_eps")
+                nc.vector.tensor_scalar_add(out=var_eps[:], in0=mean_var[:, 1:2], scalar1=EPS)
+                rstd = inverse_sqrt(var_eps, "alpha_rstd")
+                mean_rstd = small("alpha_mean_rstd")
+                nc.scalar.mul(out=mean_rstd[:], in_=mean_var[:, 0:1], mul=rstd[:])
+                shift = small("alpha_shift")
+                nc.scalar.mul(out=shift[:], in_=mean_rstd[:], mul=-1.0)
+                nc.scalar.activation(
+                    out=normed[s][:, j, :], in_=bank[:], func=ACT.Identity,
+                    bias=shift[:], scale=rstd[:],
+                )
+
+        def sigmoid(s):
+            gate_t[s] = sb.tile([P, CT, GROUP], F32, tag="gate_t", bufs=2, name="gate_t")
+            for ct in range(CT):
+                bank = psum.tile([P, GROUP], F32, tag="tp")
+                for j in range(J):
+                    nc.tensor.transpose(
+                        bank[:, j * P : (j + 1) * P],
+                        normed[s][:, j, ct * P : (ct + 1) * P],
+                        ident_f32[:],
+                    )
+                nc.scalar.activation(
+                    out=gate_t[s][:, ct, :], in_=bank[:], func=ACT.Sigmoid,
+                    bias=b_att_col[:, ct : ct + 1], scale=g_att_col[:, ct : ct + 1],
+                )
+
+        def msg_project(s):
+            msg_banks[s] = transposed_product(wm, hm_q[s])
+
+        def gate(s):
+            gated_t = sb.tile([P, CT, GROUP], BF16, tag="gated_t", bufs=2)
+            for ct in range(CT):
+                nc.vector.scalar_tensor_tensor(
+                    out=gated_t[:, ct, :], in0=msg_banks[s][ct][:], scalar=bm2_col[:, ct : ct + 1],
+                    in1=gate_t[s][:, ct, :], op0=ALU.add, op1=ALU.mult,
+                )
+            grouped = sb.tile([P, GROUP, PACK], BF16, tag="gated_grouped", bufs=2, align_bytes=64)
+            nc.vector.tensor_copy(out=grouped[:], in_=gated_t[:].rearrange("p t n -> p n t"))
+            gated_q[s] = quantise(grouped[:].rearrange("p n t -> p (n t)"), GROUP, "gated", T + 1)
+
+        def edge_plus_b_bn(g):
+            residual[g] = sb.tile([P, J, C], F32, tag="residual", name="residual")
+            for j in range(J):
+                nc.gpsimd.tensor_tensor(
+                    out=residual[g][:, j, :], in0=edge_rows[g][:, j, :], in1=b_bn_bc[:], op=ALU.add
+                )
+
+        def u_and_statistics(g):
+            v = sb.tile([P, J, C], F32, tag="v_rows", bufs=2)
+            squares = sb.tile([P, J, C], F32, tag="squares")
+            v_rows[g] = v
+            v_stats[g] = []
+            for j in range(J):
+                acc = psum.tile([P, C], F32, tag="mx")
+                for t in range(T):
+                    matmul_mx(
+                        acc[:], columns(gated_q[T * g + t], j), whole(wc),
+                        start=(t == 0), stop=(t == T - 1),
+                    )
+                total = small("u_total")
+                nc.vector.scalar_tensor_tensor(
+                    out=v[:, j, :], in0=acc[:], scalar=1.0, in1=bc_sum[:],
+                    op0=ALU.mult, op1=ALU.add, accum_out=total[:],
+                )
+                neg_mean = small("u_neg_mean")
+                nc.scalar.mul(out=neg_mean[:], in_=total[:], mul=-1.0 / C)
+                deviation = small("u_deviation")
+                nc.scalar.activation(
+                    out=squares[:, j, :], in_=v[:, j, :], func=ACT.Square,
+                    bias=neg_mean[:], accum_out=deviation[:],
+                )
+                var_eps = small("u_var_eps")
+                nc.gpsimd.tensor_scalar(
+                    out=var_eps[:], in0=deviation[:], scalar1=1.0 / C, scalar2=EPS,
+                    op0=ALU.mult, op1=ALU.add,
+                )
+                v_stats[g].append((neg_mean, inverse_sqrt(var_eps, "u_rstd")))
+
+        def add_norm_to_edge(g):
+            v = v_rows[g]
+            s = sb.tile([P, J, C], F32, tag="softplus", bufs=2)
+            for pair in ((0, 1), (2, 3)):
+                for j in pair:
+                    neg_mean, rstd = v_stats[g][j]
+                    nc.vector.scalar_tensor_tensor(
+                        out=v[:, j, :], in0=v[:, j, :], scalar=neg_mean[:], in1=g_bn_bc[:],
+                        op0=ALU.add, op1=ALU.mult,
+                    )
+                for j in pair:
+                    neg_mean, rstd = v_stats[g][j]
+                    nc.vector.scalar_tensor_tensor(
+                        out=v[:, j, :], in0=v[:, j, :], scalar=rstd[:], in1=residual[g][:, j, :],
+                        op0=ALU.mult, op1=ALU.add,
+                    )
+                for j in pair:
+                    nc.scalar.activation(out=s[:, j, :], in_=v[:, j, :], func=ACT.Abs)
+                for j in pair:
+                    nc.scalar.activation(out=s[:, j, :], in_=s[:, j, :], func=ACT.Sigmoid)
+            softplus[g] = s
+
+        def logarithm(g):
+            for j in range(J):
+                nc.scalar.activation(out=softplus[g][:, j, :], in_=softplus[g][:, j, :], func=ACT.Ln)
+
+        def store(g):
+            for j in range(J):
+                nc.vector.scalar_tensor_tensor(
+                    out=softplus[g][:, j, :], in0=v_rows[g][:, j, :], scalar=0.0,
+                    in1=softplus[g][:, j, :], op0=ALU.max, op1=ALU.subtract,
+                )
+                nc.sync.dma_start(out=out_v[g][:, j, :], in_=softplus[g][:, j, :])
+
+        load_step(-1)
+        wq_raw = load_first_stage_weight(Wq)
+        wk_raw = load_first_stage_weight(Wk2)
+        load_step(0)
+        transpose_step(-1)
+        transpose_step(0)
+        wq = quantise_weight(wq_raw, "wq")
+        quantise_step(-1)
+        q_project(0)
+        wk = quantise_weight(wk_raw, "wk")
+        quantise_step(0)
+        k_project(0)
+        wm_raw = load_first_stage_weight(Wm2)
+        load_step(1)
+        wc_raw = load_second_stage_weight(Wc)
+        load_step(2)
+        bc_bc = sb.tile([P, C], BF16)
+        nc.sync.dma_start(out=bc_bc[:], in_=bc.partition_broadcast(P))
+        g_bn_bc = sb.tile([P, C], BF16)
+        nc.sync.dma_start(out=g_bn_bc[:], in_=g_bn.partition_broadcast(P))
+        b_bn_bc = sb.tile([P, C], BF16)
+        nc.sync.dma_start(out=b_bn_bc[:], in_=b_bn.partition_broadcast(P))
+        transpose_step(1)
+        alpha(0)
+
+        GROUP_END_PARTS = 4
+        for i in range(N_STEPS - 1 + GATE_LAG + GROUP_END_PARTS):
+            complete = [T * g + T - 1 + GATE_LAG for g in range(N_GROUPS)]
+            if is_step(i - GATE_LAG):
+                msg_project(i - GATE_LAG)
+            quantise_step(i + QUANTISE_AHEAD)
+            if is_step(i):
+                normalise(i)
+            for g in range(N_GROUPS):
+                if i == complete[g] - 1:
+                    edge_plus_b_bn(g)
+            if i == 0:
+                wm = quantise_weight(wm_raw, "wm")
+                wc = quantise_weight(wc_raw, "wc")
+                bc_sum = sb.tile([P, C], F32)
+                nc.vector.tensor_scalar_mul(out=bc_sum[:], in0=bc_bc[:], scalar1=float(T))
+            if is_step(i - GATE_LAG):
+                gate(i - GATE_LAG)
+            transpose_step(i + TRANSPOSE_AHEAD)
+            load_step(i + LOAD_AHEAD)
+            for g in range(N_GROUPS):
+                if i == complete[g]:
+                    u_and_statistics(g)
+            if starts_group(i + QUANTISE_AHEAD + 1):
+                q_project((i + QUANTISE_AHEAD + 1) // T)
+            if is_step(i + 1):
+                k_project(i + 1)
+            if is_step(i):
+                sigmoid(i)
+            for g in range(N_GROUPS):
+                if i == complete[g] + 1:
+                    add_norm_to_edge(g)
+                if i == complete[g] + 2:
+                    logarithm(g)
+                if i == complete[g] + 3:
+                    store(g)
+            if is_step(i + 1):
+                alpha(i + 1)

@@ -21,12 +21,14 @@ J = GROUP // P
 CT = C // P
 N_STEPS = N_GROUPS * T
 EPS = 1e-5
+RUN = 4
 STAT_BUFS = 2 * J
 
 LOAD_AHEAD = 3
 TRANSPOSE_AHEAD = 2
 QUANTISE_AHEAD = 1
-GATE_LAG = 1
+NORMALISE_LAG = 1
+GATE_LAG = 2
 
 FLOPS = 2 * C * C * (E + 3 * E * T)
 
@@ -63,6 +65,12 @@ def tile_comformerconvedgelayer_pb_t_kernel(
             nc.vector.quantize_mx(out=codes[:].bitcast(FP8X4), scales=scales[:], in_=grouped)
             return codes, scales
 
+        def regroup(grouped, planes):
+            nc.vector.tensor_copy(
+                out=grouped[:].rearrange("p (c i) t -> p c t i", i=RUN),
+                in_=planes[:].rearrange("p t (c i) -> p c t i", i=RUN),
+            )
+
         def transposed_product(weight, moving):
             banks = []
             for ct in range(CT):
@@ -74,16 +82,20 @@ def tile_comformerconvedgelayer_pb_t_kernel(
         def small(tag):
             return sb.tile([P, 1], F32, tag=tag, bufs=STAT_BUFS, name=tag)
 
-        def inverse_sqrt(x, tag):
-            y = small(tag)
-            nc.gpsimd.tensor_tensor(out=y[:], in0=x[:], in1=neg_half[:], op=ALU.pow)
-            return y
+        def inverse_std(square_sum, divisor, tag):
+            var_eps = small(tag + "_var_eps")
+            nc.gpsimd.tensor_scalar(
+                out=var_eps[:], in0=square_sum, scalar1=divisor, scalar2=EPS, op0=ALU.mult, op1=ALU.add
+            )
+            rstd = small(tag + "_rstd")
+            nc.gpsimd.tensor_tensor(out=rstd[:], in0=var_eps[:], in1=neg_half[:, 0:1], op=ALU.pow)
+            return rstd
 
         ident_f32 = sb.tile([P, P], F32)
         make_identity(nc, ident_f32[:])
         ident_bf16 = sb.tile([P, P], BF16)
         make_identity(nc, ident_bf16[:])
-        neg_half = sb.tile([P, 1], F32)
+        neg_half = sb.tile([P, J], F32)
         nc.vector.memset(neg_half[:], -0.5)
 
         vec_rows = sb.tile([P, P], BF16)
@@ -121,7 +133,7 @@ def tile_comformerconvedgelayer_pb_t_kernel(
 
         def quantise_weight(raw, name):
             grouped = sb.tile([P, C, PACK], BF16, tag="w_grouped", align_bytes=64)
-            nc.vector.tensor_copy(out=grouped[:], in_=raw[:].rearrange("p t c -> p c t"))
+            regroup(grouped, raw)
             return quantise(grouped[:].rearrange("p c t -> p (c t)"), C, name, 1)
 
         edge_v = edge.rearrange("(g p j) c -> g p j c", g=N_GROUPS, p=P)
@@ -133,6 +145,7 @@ def tile_comformerconvedgelayer_pb_t_kernel(
         hk_rows, hk_grouped, hk_q, k_banks = {}, {}, {}, {}
         hm_rows, hm_grouped, hm_q, msg_banks = {}, {}, {}, {}
         alpha_t, normed, gate_t, gated_q = {}, {}, {}, {}
+        gated_t, gated_grouped, alpha_stats = {}, {}, {}
         v_rows, v_stats, residual, softplus = {}, {}, {}, {}
 
         def load_rows(view, tag, bufs):
@@ -155,7 +168,7 @@ def tile_comformerconvedgelayer_pb_t_kernel(
                 hm_rows[s] = load_rows(hm_v[g][:, :, t, :], "hm_rows", LOAD_AHEAD)
 
         def transpose_rows(rows):
-            grouped = sb.tile([P, PACK * GROUP], BF16, tag="x_grouped", bufs=3, align_bytes=64)
+            grouped = sb.tile([P, PACK * GROUP], BF16, tag="x_grouped", bufs=5, align_bytes=64)
             grouped_words = grouped[:].bitcast(F32).rearrange("p (n u) -> p n u", u=2)
             for half in range(2):
                 bank = psum.tile([P, 2, 2 * P], F32, tag="tp")
@@ -180,11 +193,16 @@ def tile_comformerconvedgelayer_pb_t_kernel(
                 hk_grouped[s] = transpose_rows(hk_rows[s])
                 hm_grouped[s] = transpose_rows(hm_rows[s])
 
-        def quantise_step(s):
+        def quantise_edge(s):
             if starts_group(s + 1):
                 edge_q[(s + 1) // T] = quantise(edge_grouped[(s + 1) // T][:], GROUP, "edge", 2)
+
+        def quantise_hk(s):
             if is_step(s):
                 hk_q[s] = quantise(hk_grouped[s][:], GROUP, "hk", 2)
+
+        def quantise_hm(s):
+            if is_step(s):
                 hm_q[s] = quantise(hm_grouped[s][:], GROUP, "hm", QUANTISE_AHEAD + GATE_LAG + 1)
 
         def q_project(g):
@@ -200,37 +218,47 @@ def tile_comformerconvedgelayer_pb_t_kernel(
             k_banks[s] = transposed_product(wk, hk_q[s])
 
         def alpha(s):
-            alpha_t[s] = sb.tile([P, CT, GROUP], F32, tag="alpha_t", name="alpha_t")
+            alpha_t[s] = sb.tile([P, CT, GROUP], F32, tag="alpha_t", bufs=2, name="alpha_t")
             for ct in range(CT):
                 nc.vector.scalar_tensor_tensor(
                     out=alpha_t[s][:, ct, :], in0=k_banks[s][ct][:], scalar=bk2_col[:, ct : ct + 1],
                     in1=q_t[s // T][:, ct, :], op0=ALU.add, op1=ALU.mult,
                 )
 
-        def normalise(s):
-            normed[s] = sb.tile([P, J, C], F32, tag="normed", bufs=2, name="normed")
+        def alpha_rows(s, j):
+            bank = psum.tile([P, C], F32, tag="tp", name="alpha_bank")
+            for ct in range(CT):
+                nc.tensor.transpose(
+                    bank[:, ct * P : (ct + 1) * P],
+                    alpha_t[s][:, ct, j * P : (j + 1) * P],
+                    ident_f32[:],
+                )
+            return bank
+
+        def statistics(s):
+            stats = sb.tile([P, J, 6], F32, tag="alpha_stats", bufs=2)
+            mean_var = sb.tile([P, J, 2], F32, tag="alpha_mean_var", bufs=2)
             for j in range(J):
-                bank = psum.tile([P, C], F32, tag="tp")
-                for ct in range(CT):
-                    nc.tensor.transpose(
-                        bank[:, ct * P : (ct + 1) * P],
-                        alpha_t[s][:, ct, j * P : (j + 1) * P],
-                        ident_f32[:],
-                    )
-                stats = sb.tile([P, 6], F32, tag="alpha_stats", bufs=STAT_BUFS)
-                nc.vector.bn_stats(out=stats[:], in_=bank[:])
-                mean_var = sb.tile([P, 2], F32, tag="alpha_mean_var", bufs=STAT_BUFS)
-                nc.vector.bn_aggr(out=mean_var[:], in_=stats[:])
-                var_eps = small("alpha_var_eps")
-                nc.vector.tensor_scalar_add(out=var_eps[:], in0=mean_var[:, 1:2], scalar1=EPS)
-                rstd = inverse_sqrt(var_eps, "alpha_rstd")
-                mean_rstd = small("alpha_mean_rstd")
-                nc.scalar.mul(out=mean_rstd[:], in_=mean_var[:, 0:1], mul=rstd[:])
-                shift = small("alpha_shift")
-                nc.scalar.mul(out=shift[:], in_=mean_rstd[:], mul=-1.0)
+                nc.vector.bn_stats(out=stats[:, j, :], in_=alpha_rows(s, j)[:])
+            for j in range(J):
+                nc.vector.bn_aggr(out=mean_var[:, j, :], in_=stats[:, j, :])
+            var_eps = sb.tile([P, J], F32, tag="alpha_var_eps", bufs=2)
+            nc.gpsimd.tensor_scalar_add(out=var_eps[:], in0=mean_var[:, :, 1], scalar1=EPS)
+            rstd = sb.tile([P, J], F32, tag="alpha_rstd", bufs=2)
+            nc.gpsimd.tensor_tensor(out=rstd[:], in0=var_eps[:], in1=neg_half[:], op=ALU.pow)
+            mean_rstd = sb.tile([P, J], F32, tag="alpha_mean_rstd", bufs=2)
+            nc.gpsimd.tensor_tensor(out=mean_rstd[:], in0=mean_var[:, :, 0], in1=rstd[:], op=ALU.mult)
+            shift = sb.tile([P, J], F32, tag="alpha_shift", bufs=2)
+            nc.gpsimd.tensor_scalar_mul(out=shift[:], in0=mean_rstd[:], scalar1=-1.0)
+            alpha_stats[s] = (rstd, shift)
+
+        def normalise(s):
+            rstd, shift = alpha_stats[s]
+            normed[s] = sb.tile([P, J, C], F32, tag="normed", bufs=1, name="normed")
+            for j in range(J):
                 nc.scalar.activation(
-                    out=normed[s][:, j, :], in_=bank[:], func=ACT.Identity,
-                    bias=shift[:], scale=rstd[:],
+                    out=normed[s][:, j, :], in_=alpha_rows(s, j)[:], func=ACT.Identity,
+                    bias=shift[:, j : j + 1], scale=rstd[:, j : j + 1],
                 )
 
         def sigmoid(s):
@@ -251,16 +279,22 @@ def tile_comformerconvedgelayer_pb_t_kernel(
         def msg_project(s):
             msg_banks[s] = transposed_product(wm, hm_q[s])
 
-        def gate(s):
-            gated_t = sb.tile([P, CT, GROUP], BF16, tag="gated_t", bufs=2)
+        def gate_multiply(s):
+            gated_t[s] = sb.tile([P, CT, GROUP], BF16, tag="gated_t", bufs=1, name="gated_t")
             for ct in range(CT):
                 nc.vector.scalar_tensor_tensor(
-                    out=gated_t[:, ct, :], in0=msg_banks[s][ct][:], scalar=bm2_col[:, ct : ct + 1],
+                    out=gated_t[s][:, ct, :], in0=msg_banks[s][ct][:], scalar=bm2_col[:, ct : ct + 1],
                     in1=gate_t[s][:, ct, :], op0=ALU.add, op1=ALU.mult,
                 )
-            grouped = sb.tile([P, GROUP, PACK], BF16, tag="gated_grouped", bufs=2, align_bytes=64)
-            nc.vector.tensor_copy(out=grouped[:], in_=gated_t[:].rearrange("p t n -> p n t"))
-            gated_q[s] = quantise(grouped[:].rearrange("p n t -> p (n t)"), GROUP, "gated", T + 1)
+
+        def gate_regroup(s):
+            gated_grouped[s] = sb.tile(
+                [P, GROUP, PACK], BF16, tag="gated_grouped", bufs=2, align_bytes=64, name="gated_grouped"
+            )
+            regroup(gated_grouped[s], gated_t[s])
+
+        def gate_quantise(s):
+            gated_q[s] = quantise(gated_grouped[s][:].rearrange("p n t -> p (n t)"), GROUP, "gated", T + 1)
 
         def edge_plus_b_bn(g):
             residual[g] = sb.tile([P, J, C], F32, tag="residual", name="residual")
@@ -271,8 +305,8 @@ def tile_comformerconvedgelayer_pb_t_kernel(
 
         def u_and_statistics(g):
             v = sb.tile([P, J, C], F32, tag="v_rows", bufs=2)
-            squares = sb.tile([P, J, C], F32, tag="squares")
             v_rows[g] = v
+            softplus[g] = sb.tile([P, J, C], F32, tag="softplus", bufs=2, name="softplus")
             v_stats[g] = []
             for j in range(J):
                 acc = psum.tile([P, C], F32, tag="mx")
@@ -290,19 +324,14 @@ def tile_comformerconvedgelayer_pb_t_kernel(
                 nc.scalar.mul(out=neg_mean[:], in_=total[:], mul=-1.0 / C)
                 deviation = small("u_deviation")
                 nc.scalar.activation(
-                    out=squares[:, j, :], in_=v[:, j, :], func=ACT.Square,
+                    out=softplus[g][:, j, :], in_=v[:, j, :], func=ACT.Square,
                     bias=neg_mean[:], accum_out=deviation[:],
                 )
-                var_eps = small("u_var_eps")
-                nc.gpsimd.tensor_scalar(
-                    out=var_eps[:], in0=deviation[:], scalar1=1.0 / C, scalar2=EPS,
-                    op0=ALU.mult, op1=ALU.add,
-                )
-                v_stats[g].append((neg_mean, inverse_sqrt(var_eps, "u_rstd")))
+                v_stats[g].append((neg_mean, inverse_std(deviation[:], 1.0 / C, "u")))
 
         def add_norm_to_edge(g):
             v = v_rows[g]
-            s = sb.tile([P, J, C], F32, tag="softplus", bufs=2)
+            s = softplus[g]
             for pair in ((0, 1), (2, 3)):
                 for j in pair:
                     neg_mean, rstd = v_stats[g][j]
@@ -320,7 +349,6 @@ def tile_comformerconvedgelayer_pb_t_kernel(
                     nc.scalar.activation(out=s[:, j, :], in_=v[:, j, :], func=ACT.Abs)
                 for j in pair:
                     nc.scalar.activation(out=s[:, j, :], in_=s[:, j, :], func=ACT.Sigmoid)
-            softplus[g] = s
 
         def logarithm(g):
             for j in range(J):
@@ -341,10 +369,11 @@ def tile_comformerconvedgelayer_pb_t_kernel(
         transpose_step(-1)
         transpose_step(0)
         wq = quantise_weight(wq_raw, "wq")
-        quantise_step(-1)
+        quantise_edge(-1)
         q_project(0)
         wk = quantise_weight(wk_raw, "wk")
-        quantise_step(0)
+        quantise_hk(0)
+        quantise_hm(0)
         k_project(0)
         wm_raw = load_first_stage_weight(Wm2)
         load_step(1)
@@ -362,32 +391,42 @@ def tile_comformerconvedgelayer_pb_t_kernel(
         GROUP_END_PARTS = 4
         for i in range(N_STEPS - 1 + GATE_LAG + GROUP_END_PARTS):
             complete = [T * g + T - 1 + GATE_LAG for g in range(N_GROUPS)]
-            if is_step(i - GATE_LAG):
-                msg_project(i - GATE_LAG)
-            quantise_step(i + QUANTISE_AHEAD)
+            gated = i - GATE_LAG
+            normal = i - NORMALISE_LAG
+            if is_step(gated):
+                msg_project(gated)
+            if is_step(gated):
+                gate_multiply(gated)
             if is_step(i):
-                normalise(i)
-            for g in range(N_GROUPS):
-                if i == complete[g] - 1:
-                    edge_plus_b_bn(g)
+                statistics(i)
+            if starts_group(i + 1):
+                q_project((i + 1) // T)
+            quantise_hk(i + QUANTISE_AHEAD)
+            if is_step(gated):
+                gate_regroup(gated)
+            quantise_hm(i + QUANTISE_AHEAD)
+            if is_step(gated):
+                gate_quantise(gated)
+            quantise_edge(i + QUANTISE_AHEAD)
             if i == 0:
                 wm = quantise_weight(wm_raw, "wm")
                 wc = quantise_weight(wc_raw, "wc")
                 bc_sum = sb.tile([P, C], F32)
                 nc.vector.tensor_scalar_mul(out=bc_sum[:], in0=bc_bc[:], scalar1=float(T))
-            if is_step(i - GATE_LAG):
-                gate(i - GATE_LAG)
+            if is_step(normal):
+                normalise(normal)
             transpose_step(i + TRANSPOSE_AHEAD)
             load_step(i + LOAD_AHEAD)
             for g in range(N_GROUPS):
+                if i == complete[g] - 1:
+                    edge_plus_b_bn(g)
+            for g in range(N_GROUPS):
                 if i == complete[g]:
                     u_and_statistics(g)
-            if starts_group(i + QUANTISE_AHEAD + 1):
-                q_project((i + QUANTISE_AHEAD + 1) // T)
             if is_step(i + 1):
                 k_project(i + 1)
-            if is_step(i):
-                sigmoid(i)
+            if is_step(normal):
+                sigmoid(normal)
             for g in range(N_GROUPS):
                 if i == complete[g] + 1:
                     add_norm_to_edge(g)

@@ -40,7 +40,6 @@ def tile_comformerconvedgelayer_pb_t_kernel(
     with ExitStack() as ctx:
         sb = ctx.enter_context(tc.tile_pool(name="sb", bufs=1))
         psum = ctx.enter_context(tc.psum_pool(name="psum", bufs=4))
-        ctx.enter_context(tc.manual_schedule())
 
         def matmul_mx(acc, stationary, moving, start=True, stop=True):
             nc.tensor.matmul_mx(

@@ -40,6 +40,7 @@ def tile_comformerconvedgelayer_pb_t_kernel(
     with ExitStack() as ctx:
         sb = ctx.enter_context(tc.tile_pool(name="sb", bufs=1))
         psum = ctx.enter_context(tc.psum_pool(name="psum", bufs=4))
+        ctx.enter_context(tc.manual_schedule())
 
         def matmul_mx(acc, stationary, moving, start=True, stop=True):
             nc.tensor.matmul_mx(
@@ -96,6 +97,7 @@ def tile_comformerconvedgelayer_pb_t_kernel(
         make_identity(nc, ident_bf16[:])
         neg_half = sb.tile([P, J], F32)
         nc.vector.memset(neg_half[:], -0.5)
+        table_warmer = sb.tile([P, 1], F32)
 
         vec_rows = sb.tile([P, P], BF16)
         nc.vector.memset(vec_rows[:], 0.0)
@@ -330,7 +332,6 @@ def tile_comformerconvedgelayer_pb_t_kernel(
 
         def add_norm_to_edge(g):
             v = v_rows[g]
-            s = softplus[g]
             for pair in ((0, 1), (2, 3)):
                 for j in pair:
                     neg_mean, rstd = v_stats[g][j]
@@ -344,6 +345,10 @@ def tile_comformerconvedgelayer_pb_t_kernel(
                         out=v[:, j, :], in0=v[:, j, :], scalar=rstd[:], in1=residual[g][:, j, :],
                         op0=ALU.mult, op1=ALU.add,
                     )
+
+        def sigmoid_of_abs(g):
+            v, s = v_rows[g], softplus[g]
+            for pair in ((0, 1), (2, 3)):
                 for j in pair:
                     nc.scalar.activation(out=s[:, j, :], in_=v[:, j, :], func=ACT.Abs)
                 for j in pair:
@@ -352,6 +357,7 @@ def tile_comformerconvedgelayer_pb_t_kernel(
         def logarithm(g):
             for j in range(J):
                 nc.scalar.activation(out=softplus[g][:, j, :], in_=softplus[g][:, j, :], func=ACT.Ln)
+            nc.scalar.activation(out=table_warmer[:], in_=neg_half[:, 0:1], func=ACT.Sigmoid)
 
         def store(g):
             for j in range(J):
@@ -396,6 +402,12 @@ def tile_comformerconvedgelayer_pb_t_kernel(
                 msg_project(gated)
             if is_step(gated):
                 gate_multiply(gated)
+            if i == 0:
+                wm = quantise_weight(wm_raw, "wm")
+            if i == 1:
+                wc = quantise_weight(wc_raw, "wc")
+                bc_sum = sb.tile([P, C], F32)
+                nc.vector.tensor_scalar_mul(out=bc_sum[:], in0=bc_bc[:], scalar1=float(T))
             if is_step(i):
                 statistics(i)
             if starts_group(i + 1):
@@ -407,11 +419,6 @@ def tile_comformerconvedgelayer_pb_t_kernel(
             if is_step(gated):
                 gate_quantise(gated)
             quantise_edge(i + QUANTISE_AHEAD)
-            if i == 0:
-                wm = quantise_weight(wm_raw, "wm")
-                wc = quantise_weight(wc_raw, "wc")
-                bc_sum = sb.tile([P, C], F32)
-                nc.vector.tensor_scalar_mul(out=bc_sum[:], in0=bc_bc[:], scalar1=float(T))
             if is_step(normal):
                 normalise(normal)
             transpose_step(i + TRANSPOSE_AHEAD)
@@ -429,6 +436,8 @@ def tile_comformerconvedgelayer_pb_t_kernel(
             for g in range(N_GROUPS):
                 if i == complete[g] + 1:
                     add_norm_to_edge(g)
+                if i == complete[g] + 1:
+                    sigmoid_of_abs(g)
                 if i == complete[g] + 2:
                     logarithm(g)
                 if i == complete[g] + 3:

@@ -147,7 +147,7 @@ def tile_comformerconvedgelayer_pb_t_kernel(
         hm_rows, hm_grouped, hm_q, msg_banks = {}, {}, {}, {}
         alpha_t, normed, gate_t, gated_q = {}, {}, {}, {}
         gated_t, gated_grouped, alpha_stats = {}, {}, {}
-        v_rows, v_stats, residual, softplus = {}, {}, {}, {}
+        v_rows, v_stats, softplus = {}, {}, {}
 
         def load_rows(view, tag, bufs):
             rows = sb.tile([P, J, C], BF16, tag=tag, bufs=bufs)
@@ -297,12 +297,11 @@ def tile_comformerconvedgelayer_pb_t_kernel(
         def gate_quantise(s):
             gated_q[s] = quantise(gated_grouped[s][:].rearrange("p n t -> p (n t)"), GROUP, "gated", T + 1)
 
-        def edge_plus_b_bn(g):
-            residual[g] = sb.tile([P, J, C], F32, tag="residual", name="residual")
-            for j in range(J):
-                nc.gpsimd.tensor_tensor(
-                    out=residual[g][:, j, :], in0=edge_rows[g][:, j, :], in1=b_bn_bc[:], op=ALU.add
-                )
+        def edge_plus_b_bn(g, j):
+            bank = psum.tile([P, C], F32, tag="tp", name="residual")
+            nc.tensor.matmul(bank[:], ident_bf16[:], edge_rows[g][:, j, :], start=True, stop=False)
+            nc.tensor.matmul(bank[:], ident_bf16[:], b_bn_bc[:], start=False, stop=True)
+            return bank
 
         def u_and_statistics(g):
             v = sb.tile([P, J, C], F32, tag="v_rows", bufs=2)
@@ -341,8 +340,9 @@ def tile_comformerconvedgelayer_pb_t_kernel(
                     )
                 for j in pair:
                     neg_mean, rstd = v_stats[g][j]
+                    residual = edge_plus_b_bn(g, j)
                     nc.vector.scalar_tensor_tensor(
-                        out=v[:, j, :], in0=v[:, j, :], scalar=rstd[:], in1=residual[g][:, j, :],
+                        out=v[:, j, :], in0=v[:, j, :], scalar=rstd[:], in1=residual[:],
                         op0=ALU.mult, op1=ALU.add,
                     )
 
@@ -423,9 +423,6 @@ def tile_comformerconvedgelayer_pb_t_kernel(
                 normalise(normal)
             transpose_step(i + TRANSPOSE_AHEAD)
             load_step(i + LOAD_AHEAD)
-            for g in range(N_GROUPS):
-                if i == complete[g] - 1:
-                    edge_plus_b_bn(g)
             for g in range(N_GROUPS):
                 if i == complete[g]:
                     u_and_statistics(g)

@@ -22,13 +22,11 @@ CT = C // P
 N_STEPS = N_GROUPS * T
 EPS = 1e-5
 RUN = 4
-STAT_BUFS = 2 * J
+STAT_BUFS = 3 * J
 
 LOAD_AHEAD = 3
 TRANSPOSE_AHEAD = 2
-QUANTISE_AHEAD = 1
-NORMALISE_LAG = 1
-GATE_LAG = 2
+GROUP_END_BUFS = 3
 
 FLOPS = 2 * C * C * (E + 3 * E * T)
 
@@ -65,6 +63,12 @@ def tile_comformerconvedgelayer_pb_t_kernel(
             nc.vector.quantize_mx(out=codes[:].bitcast(FP8X4), scales=scales[:], in_=grouped)
             return codes, scales
 
+        def gpsimd_regroup(grouped, planes):
+            nc.gpsimd.tensor_scalar(
+                out=grouped[:], in0=planes[:].rearrange("p t n -> p n t"),
+                scalar1=1.0, scalar2=0.0, op0=ALU.mult, op1=ALU.add,
+            )
+
         def regroup(grouped, planes):
             nc.vector.tensor_copy(
                 out=grouped[:].rearrange("p (c i) t -> p c t i", i=RUN),
@@ -82,15 +86,6 @@ def tile_comformerconvedgelayer_pb_t_kernel(
         def small(tag):
             return sb.tile([P, 1], F32, tag=tag, bufs=STAT_BUFS, name=tag)
 
-        def inverse_std(square_sum, divisor, tag):
-            var_eps = small(tag + "_var_eps")
-            nc.gpsimd.tensor_scalar(
-                out=var_eps[:], in0=square_sum, scalar1=divisor, scalar2=EPS, op0=ALU.mult, op1=ALU.add
-            )
-            rstd = small(tag + "_rstd")
-            nc.gpsimd.tensor_tensor(out=rstd[:], in0=var_eps[:], in1=neg_half[:, 0:1], op=ALU.pow)
-            return rstd
-
         ident_f32 = sb.tile([P, P], F32)
         make_identity(nc, ident_f32[:])
         ident_bf16 = sb.tile([P, P], BF16)
@@ -98,24 +93,8 @@ def tile_comformerconvedgelayer_pb_t_kernel(
         neg_half = sb.tile([P, J], F32)
         nc.vector.memset(neg_half[:], -0.5)
         table_warmer = sb.tile([P, 1], F32)
-
-        vec_rows = sb.tile([P, P], BF16)
-        nc.vector.memset(vec_rows[:], 0.0)
-        for v, vec in enumerate((bq, bk2, bm2, g_att, b_att)):
-            nc.sync.dma_start(
-                out=vec_rows[v * CT : (v + 1) * CT, :], in_=vec.rearrange("(t p) -> t p", p=P)
-            )
-        cols_ps = psum.tile([P, P], BF16, tag="tp")
-        nc.tensor.transpose(cols_ps[:], vec_rows[:], ident_bf16[:])
-        cols = sb.tile([P, P], F32)
-        nc.vector.tensor_copy(out=cols[:], in_=cols_ps[:])
-        bk2_col = cols[:, 1 * CT : 2 * CT]
-        bm2_col = cols[:, 2 * CT : 3 * CT]
-        g_att_col = cols[:, 3 * CT : 4 * CT]
-        b_att_col = cols[:, 4 * CT : 5 * CT]
-        inv_sqrt_c = 1.0 / math.sqrt(C)
-        bq_scaled_col = sb.tile([P, CT], F32)
-        nc.vector.tensor_scalar_mul(out=bq_scaled_col[:], in0=cols[:, 0:CT], scalar1=inv_sqrt_c)
+        floor = sb.tile([P, 1], F32)
+        nc.vector.memset(floor[:], 2.0 ** -60)
 
         def load_weight(w_view, split):
             raw = sb.tile([P, PACK, C], BF16, tag="w_raw", bufs=2)
@@ -132,9 +111,12 @@ def tile_comformerconvedgelayer_pb_t_kernel(
                 w.rearrange("(u e p) c -> p u e c", u=2, e=2, p=P), "p (u e) c -> p u e c"
             )
 
-        def quantise_weight(raw, name):
-            grouped = sb.tile([P, C, PACK], BF16, tag="w_grouped", align_bytes=64)
-            regroup(grouped, raw)
+        def group_weight(raw, copy):
+            grouped = sb.tile([P, C, PACK], BF16, tag="w_grouped", bufs=2, align_bytes=64)
+            copy(grouped, raw)
+            return grouped
+
+        def quantise_weight(grouped, name):
             return quantise(grouped[:].rearrange("p c t -> p (c t)"), C, name, 1)
 
         edge_v = edge.rearrange("(g p j) c -> g p j c", g=N_GROUPS, p=P)
@@ -145,9 +127,9 @@ def tile_comformerconvedgelayer_pb_t_kernel(
         edge_rows, edge_grouped, edge_q, q_t = {}, {}, {}, {}
         hk_rows, hk_grouped, hk_q, k_banks = {}, {}, {}, {}
         hm_rows, hm_grouped, hm_q, msg_banks = {}, {}, {}, {}
-        alpha_t, normed, gate_t, gated_q = {}, {}, {}, {}
-        gated_t, gated_grouped, alpha_stats = {}, {}, {}
-        v_rows, v_stats, softplus = {}, {}, {}
+        alpha_t, rows_t, gate_t, gated_q = {}, {}, {}, {}
+        gated_t, gated_grouped, alpha_bn, alpha_stats = {}, {}, {}, {}
+        v_rows, v_stats, softplus, u_banks = {}, {}, {}, {}
 
         def load_rows(view, tag, bufs):
             rows = sb.tile([P, J, C], BF16, tag=tag, bufs=bufs)
@@ -169,7 +151,7 @@ def tile_comformerconvedgelayer_pb_t_kernel(
                 hm_rows[s] = load_rows(hm_v[g][:, :, t, :], "hm_rows", LOAD_AHEAD)
 
         def transpose_rows(rows):
-            grouped = sb.tile([P, PACK * GROUP], BF16, tag="x_grouped", bufs=5, align_bytes=64)
+            grouped = sb.tile([P, PACK * GROUP], BF16, tag="x_grouped", bufs=4, align_bytes=64)
             grouped_words = grouped[:].bitcast(F32).rearrange("p (n u) -> p n u", u=2)
             for half in range(2):
                 bank = psum.tile([P, 2, 2 * P], F32, tag="tp")
@@ -187,11 +169,16 @@ def tile_comformerconvedgelayer_pb_t_kernel(
                 )
             return grouped
 
-        def transpose_step(s):
+        def transpose_edge(s):
             if starts_group(s + 1):
                 edge_grouped[(s + 1) // T] = transpose_rows(edge_rows[(s + 1) // T])
+
+        def transpose_hk(s):
             if is_step(s):
                 hk_grouped[s] = transpose_rows(hk_rows[s])
+
+        def transpose_hm(s):
+            if is_step(s):
                 hm_grouped[s] = transpose_rows(hm_rows[s])
 
         def quantise_edge(s):
@@ -204,7 +191,7 @@ def tile_comformerconvedgelayer_pb_t_kernel(
 
         def quantise_hm(s):
             if is_step(s):
-                hm_q[s] = quantise(hm_grouped[s][:], GROUP, "hm", QUANTISE_AHEAD + GATE_LAG + 1)
+                hm_q[s] = quantise(hm_grouped[s][:], GROUP, "hm", 3)
 
         def q_project(g):
             banks = transposed_product(wq, edge_q[g])
@@ -215,61 +202,71 @@ def tile_comformerconvedgelayer_pb_t_kernel(
                     bias=bq_scaled_col[:, ct : ct + 1], scale=inv_sqrt_c,
                 )
 
-        def k_project(s):
-            k_banks[s] = transposed_product(wk, hk_q[s])
+        def product(banks, s, weight, moving, cts):
+            for ct in cts:
+                banks[s, ct] = psum.tile([P, GROUP], F32, tag="mx", name="acc")
+                matmul_mx(banks[s, ct][:], columns(weight, ct), whole(moving))
 
-        def alpha(s):
-            alpha_t[s] = sb.tile([P, CT, GROUP], F32, tag="alpha_t", bufs=2, name="alpha_t")
-            for ct in range(CT):
+        def k_project(s, cts):
+            if is_step(s):
+                product(k_banks, s, wk, hk_q[s], cts)
+
+        def alpha(s, cts):
+            if not is_step(s):
+                return
+            if 0 in cts:
+                alpha_t[s] = sb.tile([P, CT, GROUP], F32, tag="alpha_t", bufs=1, name="alpha_t")
+            for ct in cts:
                 nc.vector.scalar_tensor_tensor(
-                    out=alpha_t[s][:, ct, :], in0=k_banks[s][ct][:], scalar=bk2_col[:, ct : ct + 1],
+                    out=alpha_t[s][:, ct, :], in0=k_banks[s, ct][:], scalar=bk2_col[:, ct : ct + 1],
                     in1=q_t[s // T][:, ct, :], op0=ALU.add, op1=ALU.mult,
                 )
 
-        def alpha_rows(s, j):
-            bank = psum.tile([P, C], F32, tag="tp", name="alpha_bank")
-            for ct in range(CT):
-                nc.tensor.transpose(
-                    bank[:, ct * P : (ct + 1) * P],
-                    alpha_t[s][:, ct, j * P : (j + 1) * P],
-                    ident_f32[:],
-                )
-            return bank
+        def alpha_rows(s, tiles):
+            if not is_step(s):
+                return
+            if 0 in tiles:
+                rows_t[s] = sb.tile([P, J, C], F32, tag="rows_t", bufs=2, name="rows_t")
+                alpha_bn[s] = sb.tile([P, J, 6], F32, tag="alpha_bn", bufs=2, name="alpha_bn")
+            for j in tiles:
+                bank = psum.tile([P, C], F32, tag="tp", name="alpha_bank")
+                for ct in range(CT):
+                    nc.tensor.transpose(
+                        bank[:, ct * P : (ct + 1) * P],
+                        alpha_t[s][:, ct, j * P : (j + 1) * P],
+                        ident_f32[:],
+                    )
+                nc.vector.bn_stats(out=alpha_bn[s][:, j, :], in_=bank[:])
+                nc.scalar.copy(out=rows_t[s][:, j, :], in_=bank[:])
 
-        def statistics(s):
-            stats = sb.tile([P, J, 6], F32, tag="alpha_stats", bufs=2)
-            mean_var = sb.tile([P, J, 2], F32, tag="alpha_mean_var", bufs=2)
-            for j in range(J):
-                nc.vector.bn_stats(out=stats[:, j, :], in_=alpha_rows(s, j)[:])
-            for j in range(J):
-                nc.vector.bn_aggr(out=mean_var[:, j, :], in_=stats[:, j, :])
-            var_eps = sb.tile([P, J], F32, tag="alpha_var_eps", bufs=2)
+        def normalise(s, tiles):
+            if not is_step(s):
+                return
+            n = len(tiles)
+            mean_var = sb.tile([P, n, 2], F32, tag="alpha_mean_var", bufs=4)
+            for x, j in enumerate(tiles):
+                nc.vector.bn_aggr(out=mean_var[:, x, :], in_=alpha_bn[s][:, j, :])
+            var_eps = sb.tile([P, n], F32, tag="alpha_var_eps", bufs=4)
             nc.gpsimd.tensor_scalar_add(out=var_eps[:], in0=mean_var[:, :, 1], scalar1=EPS)
-            rstd = sb.tile([P, J], F32, tag="alpha_rstd", bufs=2)
-            nc.gpsimd.tensor_tensor(out=rstd[:], in0=var_eps[:], in1=neg_half[:], op=ALU.pow)
-            mean_rstd = sb.tile([P, J], F32, tag="alpha_mean_rstd", bufs=2)
-            nc.gpsimd.tensor_tensor(out=mean_rstd[:], in0=mean_var[:, :, 0], in1=rstd[:], op=ALU.mult)
-            shift = sb.tile([P, J], F32, tag="alpha_shift", bufs=2)
-            nc.gpsimd.tensor_scalar_mul(out=shift[:], in0=mean_rstd[:], scalar1=-1.0)
-            alpha_stats[s] = (rstd, shift)
-
-        def normalise(s):
-            rstd, shift = alpha_stats[s]
-            normed[s] = sb.tile([P, J, C], F32, tag="normed", bufs=1, name="normed")
-            for j in range(J):
-                nc.scalar.activation(
-                    out=normed[s][:, j, :], in_=alpha_rows(s, j)[:], func=ACT.Identity,
-                    bias=shift[:, j : j + 1], scale=rstd[:, j : j + 1],
+            rstd = sb.tile([P, n], F32, tag="alpha_rstd", bufs=4)
+            nc.gpsimd.tensor_tensor(out=rstd[:], in0=var_eps[:], in1=neg_half[:, 0:n], op=ALU.pow)
+            for x, j in enumerate(tiles):
+                nc.gpsimd.tensor_scalar(
+                    out=rows_t[s][:, j, :], in0=rows_t[s][:, j, :], scalar1=mean_var[:, x, 0:1],
+                    scalar2=rstd[:, x : x + 1], op0=ALU.subtract, op1=ALU.mult,
                 )
 
-        def sigmoid(s):
-            gate_t[s] = sb.tile([P, CT, GROUP], F32, tag="gate_t", bufs=2, name="gate_t")
-            for ct in range(CT):
+        def sigmoid(s, cts):
+            if not is_step(s):
+                return
+            if 0 in cts:
+                gate_t[s] = sb.tile([P, CT, GROUP], F32, tag="gate_t", bufs=1, name="gate_t")
+            for ct in cts:
                 bank = psum.tile([P, GROUP], F32, tag="tp")
                 for j in range(J):
                     nc.tensor.transpose(
                         bank[:, j * P : (j + 1) * P],
-                        normed[s][:, j, ct * P : (ct + 1) * P],
+                        rows_t[s][:, j, ct * P : (ct + 1) * P],
                         ident_f32[:],
                     )
                 nc.scalar.activation(
@@ -277,25 +274,75 @@ def tile_comformerconvedgelayer_pb_t_kernel(
                     bias=b_att_col[:, ct : ct + 1], scale=g_att_col[:, ct : ct + 1],
                 )
 
-        def msg_project(s):
-            msg_banks[s] = transposed_product(wm, hm_q[s])
+        def msg_project(s, cts):
+            if is_step(s):
+                product(msg_banks, s, wm, hm_q[s], cts)
 
-        def gate_multiply(s):
-            gated_t[s] = sb.tile([P, CT, GROUP], BF16, tag="gated_t", bufs=1, name="gated_t")
-            for ct in range(CT):
+        def gate_multiply(s, cts):
+            if not is_step(s):
+                return
+            if 0 in cts:
+                gated_t[s] = sb.tile([P, CT, GROUP], BF16, tag="gated_t", bufs=2, name="gated_t")
+            for ct in cts:
                 nc.vector.scalar_tensor_tensor(
-                    out=gated_t[s][:, ct, :], in0=msg_banks[s][ct][:], scalar=bm2_col[:, ct : ct + 1],
+                    out=gated_t[s][:, ct, :], in0=msg_banks[s, ct][:], scalar=bm2_col[:, ct : ct + 1],
                     in1=gate_t[s][:, ct, :], op0=ALU.add, op1=ALU.mult,
                 )
 
-        def gate_regroup(s):
+        def gate_regroup(s, on_gpsimd):
+            if not is_step(s):
+                return
             gated_grouped[s] = sb.tile(
                 [P, GROUP, PACK], BF16, tag="gated_grouped", bufs=2, align_bytes=64, name="gated_grouped"
             )
-            regroup(gated_grouped[s], gated_t[s])
+            if on_gpsimd:
+                nc.gpsimd.tensor_scalar(
+                    out=gated_grouped[s][:], in0=gated_t[s][:].rearrange("p t n -> p n t"),
+                    scalar1=1.0, scalar2=0.0, op0=ALU.mult, op1=ALU.add,
+                )
+            else:
+                regroup(gated_grouped[s], gated_t[s])
 
         def gate_quantise(s):
-            gated_q[s] = quantise(gated_grouped[s][:].rearrange("p n t -> p (n t)"), GROUP, "gated", T + 1)
+            if is_step(s):
+                gated_q[s] = quantise(gated_grouped[s][:].rearrange("p n t -> p (n t)"), GROUP, "gated", T + 1)
+
+        def u_product(g, j, directions):
+            if 0 in directions:
+                u_banks[g, j] = psum.tile([P, C], F32, tag="mx", name="u_bank")
+            for t in directions:
+                matmul_mx(
+                    u_banks[g, j][:], columns(gated_q[T * g + t], j), whole(wc),
+                    start=(t == 0), stop=(t == T - 1),
+                )
+
+        def u_statistics(g, j):
+            if j == 0:
+                v_rows[g] = sb.tile([P, J, C], F32, tag="v_rows", bufs=GROUP_END_BUFS, name="v_rows")
+                softplus[g] = sb.tile([P, J, C], F32, tag="softplus", bufs=GROUP_END_BUFS, name="softplus")
+            v = v_rows[g]
+            mean = small("u_mean")
+            nc.vector.scalar_tensor_tensor(
+                out=v[:, j, :], in0=u_banks[g, j][:], scalar=1.0 / C, in1=bc_sum[:],
+                op0=ALU.mult, op1=ALU.add, accum_out=mean[:],
+            )
+            deviation = small("u_deviation")
+            nc.scalar.activation(
+                out=softplus[g][:, j, :], in_=v[:, j, :], func=ACT.Square,
+                scale=-float(C), bias=mean[:], accum_out=deviation[:],
+            )
+            v_mean = small("u_v_mean")
+            nc.gpsimd.tensor_scalar(
+                out=v_mean[:], in0=mean[:], scalar1=1.0 / C, scalar2=0.0, op0=ALU.mult, op1=ALU.add
+            )
+            var_eps = small("u_var_eps")
+            nc.gpsimd.tensor_scalar(
+                out=var_eps[:], in0=deviation[:], scalar1=C ** -3.0, scalar2=EPS * C ** -2.0,
+                op0=ALU.mult, op1=ALU.add,
+            )
+            rstd = small("u_rstd")
+            nc.gpsimd.tensor_tensor(out=rstd[:], in0=var_eps[:], in1=neg_half[:, 0:1], op=ALU.pow)
+            v_stats[g, j] = (v_mean, rstd)
 
         def edge_plus_b_bn(g, j):
             bank = psum.tile([P, C], F32, tag="tp", name="residual")
@@ -303,85 +350,82 @@ def tile_comformerconvedgelayer_pb_t_kernel(
             nc.tensor.matmul(bank[:], ident_bf16[:], b_bn_bc[:], start=False, stop=True)
             return bank
 
-        def u_and_statistics(g):
-            v = sb.tile([P, J, C], F32, tag="v_rows", bufs=2)
-            v_rows[g] = v
-            softplus[g] = sb.tile([P, J, C], F32, tag="softplus", bufs=2, name="softplus")
-            v_stats[g] = []
-            for j in range(J):
-                acc = psum.tile([P, C], F32, tag="mx")
-                for t in range(T):
-                    matmul_mx(
-                        acc[:], columns(gated_q[T * g + t], j), whole(wc),
-                        start=(t == 0), stop=(t == T - 1),
-                    )
-                total = small("u_total")
-                nc.vector.scalar_tensor_tensor(
-                    out=v[:, j, :], in0=acc[:], scalar=1.0, in1=bc_sum[:],
-                    op0=ALU.mult, op1=ALU.add, accum_out=total[:],
-                )
-                neg_mean = small("u_neg_mean")
-                nc.scalar.mul(out=neg_mean[:], in_=total[:], mul=-1.0 / C)
-                deviation = small("u_deviation")
-                nc.scalar.activation(
-                    out=softplus[g][:, j, :], in_=v[:, j, :], func=ACT.Square,
-                    bias=neg_mean[:], accum_out=deviation[:],
-                )
-                v_stats[g].append((neg_mean, inverse_std(deviation[:], 1.0 / C, "u")))
-
-        def add_norm_to_edge(g):
+        def scale_deviation(g, tiles):
             v = v_rows[g]
-            for pair in ((0, 1), (2, 3)):
-                for j in pair:
-                    neg_mean, rstd = v_stats[g][j]
-                    nc.vector.scalar_tensor_tensor(
-                        out=v[:, j, :], in0=v[:, j, :], scalar=neg_mean[:], in1=g_bn_bc[:],
-                        op0=ALU.add, op1=ALU.mult,
-                    )
-                for j in pair:
-                    neg_mean, rstd = v_stats[g][j]
-                    residual = edge_plus_b_bn(g, j)
-                    nc.vector.scalar_tensor_tensor(
-                        out=v[:, j, :], in0=v[:, j, :], scalar=rstd[:], in1=residual[:],
-                        op0=ALU.mult, op1=ALU.add,
-                    )
+            for j in tiles:
+                nc.vector.scalar_tensor_tensor(
+                    out=v[:, j, :], in0=v[:, j, :], scalar=v_stats[g, j][0][:], in1=g_bn_bc[:],
+                    op0=ALU.subtract, op1=ALU.mult,
+                )
 
-        def sigmoid_of_abs(g):
-            v, s = v_rows[g], softplus[g]
-            for pair in ((0, 1), (2, 3)):
-                for j in pair:
-                    nc.scalar.activation(out=s[:, j, :], in_=v[:, j, :], func=ACT.Abs)
-                for j in pair:
-                    nc.scalar.activation(out=s[:, j, :], in_=s[:, j, :], func=ACT.Sigmoid)
+        def add_edge(g, tiles):
+            v = v_rows[g]
+            for j in tiles:
+                residual = edge_plus_b_bn(g, j)
+                nc.vector.scalar_tensor_tensor(
+                    out=v[:, j, :], in0=v[:, j, :], scalar=v_stats[g, j][1][:], in1=residual[:],
+                    op0=ALU.mult, op1=ALU.add,
+                )
 
-        def logarithm(g):
-            for j in range(J):
-                nc.scalar.activation(out=softplus[g][:, j, :], in_=softplus[g][:, j, :], func=ACT.Ln)
+        def sigmoid_of_minus(g, tiles):
+            for j in tiles:
+                nc.scalar.activation(
+                    out=softplus[g][:, j, :], in_=v_rows[g][:, j, :], func=ACT.Sigmoid, scale=-1.0
+                )
+
+        def logarithm(g, tiles):
+            for j in tiles:
+                nc.scalar.activation(
+                    out=softplus[g][:, j, :], in_=softplus[g][:, j, :], func=ACT.Ln, bias=floor[:]
+                )
+
+        def bring_back_sigmoid():
             nc.scalar.activation(out=table_warmer[:], in_=neg_half[:, 0:1], func=ACT.Sigmoid)
 
-        def store(g):
-            for j in range(J):
+        def store(g, tiles):
+            for j in tiles:
                 nc.vector.scalar_tensor_tensor(
-                    out=softplus[g][:, j, :], in0=v_rows[g][:, j, :], scalar=0.0,
-                    in1=softplus[g][:, j, :], op0=ALU.max, op1=ALU.subtract,
+                    out=softplus[g][:, j, :], in0=softplus[g][:, j, :], scalar=-1.0,
+                    in1=v_rows[g][:, j, :], op0=ALU.mult, op1=ALU.max,
                 )
                 nc.sync.dma_start(out=out_v[g][:, j, :], in_=softplus[g][:, j, :])
 
+        ALL, LOW, HIGH = range(J), (0, 1), (2, 3)
         load_step(-1)
         wq_raw = load_first_stage_weight(Wq)
+        vec_rows = sb.tile([P, P], BF16)
+        nc.vector.memset(vec_rows[:], 0.0)
+        for v, vec in enumerate((bq, bk2, bm2, g_att, b_att)):
+            nc.sync.dma_start(
+                out=vec_rows[v * CT : (v + 1) * CT, :], in_=vec.rearrange("(t p) -> t p", p=P)
+            )
+        cols_ps = psum.tile([P, P], BF16, tag="tp")
+        nc.tensor.transpose(cols_ps[:], vec_rows[:], ident_bf16[:])
+        cols = sb.tile([P, P], F32)
+        nc.vector.tensor_copy(out=cols[:], in_=cols_ps[:])
+        bk2_col = cols[:, 1 * CT : 2 * CT]
+        bm2_col = cols[:, 2 * CT : 3 * CT]
+        g_att_col = cols[:, 3 * CT : 4 * CT]
+        b_att_col = cols[:, 4 * CT : 5 * CT]
+        inv_sqrt_c = 1.0 / math.sqrt(C)
+        bq_scaled_col = sb.tile([P, CT], F32)
+        nc.vector.tensor_scalar_mul(out=bq_scaled_col[:], in0=cols[:, 0:CT], scalar1=inv_sqrt_c)
+
+        hk_rows[0] = load_rows(hk_v[0][:, :, 0, :], "hk_rows", LOAD_AHEAD)
         wk_raw = load_first_stage_weight(Wk2)
-        load_step(0)
-        transpose_step(-1)
-        transpose_step(0)
-        wq = quantise_weight(wq_raw, "wq")
+        hm_rows[0] = load_rows(hm_v[0][:, :, 0, :], "hm_rows", LOAD_AHEAD)
+        transpose_edge(-1)
+        wq_grouped = group_weight(wq_raw, regroup)
         quantise_edge(-1)
+        wq = quantise_weight(wq_grouped, "wq")
+        transpose_hk(0)
         q_project(0)
-        wk = quantise_weight(wk_raw, "wk")
+        wk_grouped = group_weight(wk_raw, regroup)
         quantise_hk(0)
-        quantise_hm(0)
-        k_project(0)
-        wm_raw = load_first_stage_weight(Wm2)
+        wk = quantise_weight(wk_grouped, "wk")
+        k_project(0, ALL)
         load_step(1)
+        wm_raw = load_first_stage_weight(Wm2)
         wc_raw = load_second_stage_weight(Wc)
         load_step(2)
         bc_bc = sb.tile([P, C], BF16)
@@ -390,54 +434,87 @@ def tile_comformerconvedgelayer_pb_t_kernel(
         nc.sync.dma_start(out=g_bn_bc[:], in_=g_bn.partition_broadcast(P))
         b_bn_bc = sb.tile([P, C], BF16)
         nc.sync.dma_start(out=b_bn_bc[:], in_=b_bn.partition_broadcast(P))
-        transpose_step(1)
-        alpha(0)
+        transpose_hm(0)
+        alpha(0, ALL)
+        transpose_hk(1)
+        transpose_hm(1)
 
-        GROUP_END_PARTS = 4
-        for i in range(N_STEPS - 1 + GATE_LAG + GROUP_END_PARTS):
-            complete = [T * g + T - 1 + GATE_LAG for g in range(N_GROUPS)]
-            gated = i - GATE_LAG
-            normal = i - NORMALISE_LAG
-            if is_step(gated):
-                msg_project(gated)
-            if is_step(gated):
-                gate_multiply(gated)
+        for i in range(N_STEPS):
+            gated = i - 1
+            ended, age = divmod(i - (T + 1), T)
+            alpha_rows(i, LOW)
+            sigmoid(gated, LOW)
+            quantise_hk(i + 1)
+            gate_quantise(gated - 1)
+            quantise_edge(i + 1)
             if i == 0:
-                wm = quantise_weight(wm_raw, "wm")
+                wm_grouped = group_weight(wm_raw, regroup)
+                quantise_hm(0)
+                wm = quantise_weight(wm_grouped, "wm")
             if i == 1:
-                wc = quantise_weight(wc_raw, "wc")
+                wc = quantise_weight(wc_grouped, "wc")
                 bc_sum = sb.tile([P, C], F32)
-                nc.vector.tensor_scalar_mul(out=bc_sum[:], in0=bc_bc[:], scalar1=float(T))
-            if is_step(i):
-                statistics(i)
+                nc.vector.tensor_scalar_mul(out=bc_sum[:], in0=bc_bc[:], scalar1=float(T) / C)
+            if ended >= 0 and age == 1:
+                scale_deviation(ended, LOW)
+            if ended >= 0 and age == 2:
+                scale_deviation(ended, HIGH)
+            normalise(i, LOW)
             if starts_group(i + 1):
                 q_project((i + 1) // T)
-            quantise_hk(i + QUANTISE_AHEAD)
-            if is_step(gated):
-                gate_regroup(gated)
-            quantise_hm(i + QUANTISE_AHEAD)
-            if is_step(gated):
-                gate_quantise(gated)
-            quantise_edge(i + QUANTISE_AHEAD)
-            if is_step(normal):
-                normalise(normal)
-            transpose_step(i + TRANSPOSE_AHEAD)
+            msg_project(gated, LOW)
+            gate_multiply(gated, LOW)
+            alpha_rows(i, HIGH)
+            sigmoid(gated, HIGH)
+            quantise_hm(i + 1)
+            normalise(i, HIGH)
+            msg_project(gated, HIGH)
+            gate_multiply(gated, HIGH)
+            gate_regroup(gated, i < N_STEPS - 1)
+            if i == 0:
+                wc_grouped = group_weight(wc_raw, gpsimd_regroup)
+            if ended >= 0 and age == 1:
+                add_edge(ended, LOW)
+                sigmoid_of_minus(ended, LOW)
+            if ended >= 0 and age == 2:
+                add_edge(ended, HIGH)
+                sigmoid_of_minus(ended, HIGH)
+            if ended >= 0 and age == 0:
+                for j in ALL:
+                    u_product(ended, j, range(T))
+                    u_statistics(ended, j)
+            k_project(i + 1, LOW)
+            transpose_edge(i + TRANSPOSE_AHEAD)
+            transpose_hk(i + TRANSPOSE_AHEAD)
+            k_project(i + 1, HIGH)
+            transpose_hm(i + TRANSPOSE_AHEAD)
             load_step(i + LOAD_AHEAD)
-            for g in range(N_GROUPS):
-                if i == complete[g]:
-                    u_and_statistics(g)
-            if is_step(i + 1):
-                k_project(i + 1)
-            if is_step(normal):
-                sigmoid(normal)
-            for g in range(N_GROUPS):
-                if i == complete[g] + 1:
-                    add_norm_to_edge(g)
-                if i == complete[g] + 1:
-                    sigmoid_of_abs(g)
-                if i == complete[g] + 2:
-                    logarithm(g)
-                if i == complete[g] + 3:
-                    store(g)
-            if is_step(i + 1):
-                alpha(i + 1)
+            alpha(i + 1, ALL)
+
+        last, g = N_STEPS - 1, N_GROUPS - 1
+        scale_deviation(g - 1, HIGH)
+        add_edge(g - 1, HIGH)
+        gate_quantise(last - 1)
+        msg_project(last, ALL)
+        sigmoid(last, ALL)
+        sigmoid_of_minus(g - 1, HIGH)
+        gate_multiply(last, ALL)
+        gate_regroup(last, False)
+        gate_quantise(last)
+        logarithm(0, ALL)
+        for j in ALL:
+            u_product(g, j, range(T - 1))
+        for j in ALL:
+            u_product(g, j, [T - 1])
+            u_statistics(g, j)
+        logarithm(1, ALL)
+        bring_back_sigmoid()
+        scale_deviation(g, LOW)
+        add_edge(g, LOW)
+        scale_deviation(g, HIGH)
+        add_edge(g, HIGH)
+        sigmoid_of_minus(g, ALL)
+        store(0, ALL)
+        store(1, ALL)
+        logarithm(g, ALL)
+        store(g, ALL)

@@ -250,10 +250,16 @@ def tile_comformerconvedgelayer_pb_t_kernel(
             nc.gpsimd.tensor_scalar_add(out=var_eps[:], in0=mean_var[:, :, 1], scalar1=EPS)
             rstd = sb.tile([P, n], F32, tag="alpha_rstd", bufs=4)
             nc.gpsimd.tensor_tensor(out=rstd[:], in0=var_eps[:], in1=neg_half[:, 0:n], op=ALU.pow)
+            neg_mean = sb.tile([P, n], F32, tag="alpha_neg_mean", bufs=4)
+            nc.gpsimd.tensor_scalar(
+                out=neg_mean[:], in0=mean_var[:, :, 0], scalar1=-1.0, scalar2=0.0, op0=ALU.mult, op1=ALU.add
+            )
+            shift = sb.tile([P, n], F32, tag="alpha_shift", bufs=4)
+            nc.gpsimd.tensor_tensor(out=shift[:], in0=neg_mean[:], in1=rstd[:], op=ALU.mult)
             for x, j in enumerate(tiles):
                 nc.gpsimd.tensor_scalar(
-                    out=rows_t[s][:, j, :], in0=rows_t[s][:, j, :], scalar1=mean_var[:, x, 0:1],
-                    scalar2=rstd[:, x : x + 1], op0=ALU.subtract, op1=ALU.mult,
+                    out=rows_t[s][:, j, :], in0=rows_t[s][:, j, :], scalar1=rstd[:, x : x + 1],
+                    scalar2=shift[:, x : x + 1], op0=ALU.mult, op1=ALU.add,
                 )
 
         def sigmoid(s, cts):

@@ -215,51 +215,69 @@ def tile_comformerconvedgelayer_pb_t_kernel(
             if not is_step(s):
                 return
             if 0 in cts:
-                alpha_t[s] = sb.tile([P, CT, GROUP], F32, tag="alpha_t", bufs=1, name="alpha_t")
+                alpha_t[s] = sb.tile([P, CT, GROUP], F32, tag="alpha_t", bufs=2, name="alpha_t")
             for ct in cts:
                 nc.vector.scalar_tensor_tensor(
                     out=alpha_t[s][:, ct, :], in0=k_banks[s, ct][:], scalar=bk2_col[:, ct : ct + 1],
                     in1=q_t[s // T][:, ct, :], op0=ALU.add, op1=ALU.mult,
                 )
 
-        def alpha_rows(s, tiles):
+        def alpha_rows(s, j):
+            bank = psum.tile([P, C], F32, tag="tp", name="alpha_bank")
+            for ct in range(CT):
+                nc.tensor.transpose(
+                    bank[:, ct * P : (ct + 1) * P],
+                    alpha_t[s][:, ct, j * P : (j + 1) * P],
+                    ident_f32[:],
+                )
+            return bank
+
+        def statistics(s, tiles):
             if not is_step(s):
                 return
             if 0 in tiles:
-                rows_t[s] = sb.tile([P, J, C], F32, tag="rows_t", bufs=2, name="rows_t")
                 alpha_bn[s] = sb.tile([P, J, 6], F32, tag="alpha_bn", bufs=2, name="alpha_bn")
             for j in tiles:
-                bank = psum.tile([P, C], F32, tag="tp", name="alpha_bank")
-                for ct in range(CT):
-                    nc.tensor.transpose(
-                        bank[:, ct * P : (ct + 1) * P],
-                        alpha_t[s][:, ct, j * P : (j + 1) * P],
-                        ident_f32[:],
-                    )
-                nc.vector.bn_stats(out=alpha_bn[s][:, j, :], in_=bank[:])
-                nc.scalar.copy(out=rows_t[s][:, j, :], in_=bank[:])
+                nc.vector.bn_stats(out=alpha_bn[s][:, j, :], in_=alpha_rows(s, j)[:])
+
+        def aggregate(s, tiles):
+            if not is_step(s):
+                return
+            if 0 in tiles:
+                alpha_stats[s] = tuple(
+                    sb.tile([P, J] + more, F32, tag="alpha_" + tag, bufs=2, name=tag)
+                    for tag, more in (("mean_var", [2]), ("var_eps", []), ("rstd", []), ("shift", []))
+                )
+            for j in tiles:
+                nc.vector.bn_aggr(out=alpha_stats[s][0][:, j, :], in_=alpha_bn[s][:, j, :])
+
+        def power(s, tiles):
+            if not is_step(s):
+                return
+            mean_var, var_eps, rs, sh = alpha_stats[s]
+            a, b = tiles[0], tiles[-1] + 1
+            nc.vector.tensor_scalar_add(out=var_eps[:, a:b], in0=mean_var[:, a:b, 1], scalar1=EPS)
+            nc.gpsimd.tensor_tensor(out=rs[:, a:b], in0=var_eps[:, a:b], in1=neg_half[:, a:b], op=ALU.pow)
+
+        def shift(s, tiles):
+            if not is_step(s):
+                return
+            mean_var, var_eps, rs, sh = alpha_stats[s]
+            a, b = tiles[0], tiles[-1] + 1
+            nc.vector.scalar_tensor_tensor(
+                out=sh[:, a:b], in0=mean_var[:, a:b, 0], scalar=-1.0, in1=rs[:, a:b], op0=ALU.mult, op1=ALU.mult
+            )
 
         def normalise(s, tiles):
             if not is_step(s):
                 return
-            n = len(tiles)
-            mean_var = sb.tile([P, n, 2], F32, tag="alpha_mean_var", bufs=4)
-            for x, j in enumerate(tiles):
-                nc.vector.bn_aggr(out=mean_var[:, x, :], in_=alpha_bn[s][:, j, :])
-            var_eps = sb.tile([P, n], F32, tag="alpha_var_eps", bufs=4)
-            nc.gpsimd.tensor_scalar_add(out=var_eps[:], in0=mean_var[:, :, 1], scalar1=EPS)
-            rstd = sb.tile([P, n], F32, tag="alpha_rstd", bufs=4)
-            nc.gpsimd.tensor_tensor(out=rstd[:], in0=var_eps[:], in1=neg_half[:, 0:n], op=ALU.pow)
-            neg_mean = sb.tile([P, n], F32, tag="alpha_neg_mean", bufs=4)
-            nc.gpsimd.tensor_scalar(
-                out=neg_mean[:], in0=mean_var[:, :, 0], scalar1=-1.0, scalar2=0.0, op0=ALU.mult, op1=ALU.add
-            )
-            shift = sb.tile([P, n], F32, tag="alpha_shift", bufs=4)
-            nc.gpsimd.tensor_tensor(out=shift[:], in0=neg_mean[:], in1=rstd[:], op=ALU.mult)
-            for x, j in enumerate(tiles):
-                nc.gpsimd.tensor_scalar(
-                    out=rows_t[s][:, j, :], in0=rows_t[s][:, j, :], scalar1=rstd[:, x : x + 1],
-                    scalar2=shift[:, x : x + 1], op0=ALU.mult, op1=ALU.add,
+            if 0 in tiles:
+                rows_t[s] = sb.tile([P, J, C], F32, tag="rows_t", bufs=1, name="rows_t")
+            for j in tiles:
+                mean_var, var_eps, rs, sh = alpha_stats[s]
+                nc.scalar.activation(
+                    out=rows_t[s][:, j, :], in_=alpha_rows(s, j)[:], func=ACT.Identity,
+                    bias=sh[:, j : j + 1], scale=rs[:, j : j + 1],
                 )
 
         def sigmoid(s, cts):
@@ -295,16 +313,18 @@ def tile_comformerconvedgelayer_pb_t_kernel(
                     in1=gate_t[s][:, ct, :], op0=ALU.add, op1=ALU.mult,
                 )
 
-        def gate_regroup(s, on_gpsimd):
+        def gate_regroup(s, engine):
             if not is_step(s):
                 return
             gated_grouped[s] = sb.tile(
                 [P, GROUP, PACK], BF16, tag="gated_grouped", bufs=2, align_bytes=64, name="gated_grouped"
             )
-            if on_gpsimd:
-                nc.gpsimd.tensor_scalar(
-                    out=gated_grouped[s][:], in0=gated_t[s][:].rearrange("p t n -> p n t"),
-                    scalar1=1.0, scalar2=0.0, op0=ALU.mult, op1=ALU.add,
+            if engine == "G":
+                gpsimd_regroup(gated_grouped[s], gated_t[s])
+            elif engine == "S":
+                nc.scalar.copy(
+                    out=gated_grouped[s][:].rearrange("p (c i) t -> p c t i", i=RUN),
+                    in_=gated_t[s][:].rearrange("p t (c i) -> p c t i", i=RUN),
                 )
             else:
                 regroup(gated_grouped[s], gated_t[s])
@@ -326,29 +346,32 @@ def tile_comformerconvedgelayer_pb_t_kernel(
             if j == 0:
                 v_rows[g] = sb.tile([P, J, C], F32, tag="v_rows", bufs=GROUP_END_BUFS, name="v_rows")
                 softplus[g] = sb.tile([P, J, C], F32, tag="softplus", bufs=GROUP_END_BUFS, name="softplus")
+                v_stats[g] = tuple(
+                    sb.tile([P, J], F32, tag="u_" + tag, bufs=2, name=tag)
+                    for tag in ("mean", "deviation", "v_mean", "var_eps", "rstd")
+                )
             v = v_rows[g]
-            mean = small("u_mean")
+            mean, deviation, v_mean, var_eps, rs = v_stats[g]
             nc.vector.scalar_tensor_tensor(
                 out=v[:, j, :], in0=u_banks[g, j][:], scalar=1.0 / C, in1=bc_sum[:],
-                op0=ALU.mult, op1=ALU.add, accum_out=mean[:],
+                op0=ALU.mult, op1=ALU.add, accum_out=mean[:, j : j + 1],
             )
-            deviation = small("u_deviation")
             nc.scalar.activation(
                 out=softplus[g][:, j, :], in_=v[:, j, :], func=ACT.Square,
-                scale=-float(C), bias=mean[:], accum_out=deviation[:],
+                scale=-float(C), bias=mean[:, j : j + 1], accum_out=deviation[:, j : j + 1],
             )
-            v_mean = small("u_v_mean")
+
+        def u_rstd(g, tiles):
+            mean, deviation, v_mean, var_eps, rs = v_stats[g]
+            a, b = tiles[0], tiles[-1] + 1
             nc.gpsimd.tensor_scalar(
-                out=v_mean[:], in0=mean[:], scalar1=1.0 / C, scalar2=0.0, op0=ALU.mult, op1=ALU.add
+                out=v_mean[:, a:b], in0=mean[:, a:b], scalar1=1.0 / C, scalar2=0.0, op0=ALU.mult, op1=ALU.add
             )
-            var_eps = small("u_var_eps")
             nc.gpsimd.tensor_scalar(
-                out=var_eps[:], in0=deviation[:], scalar1=C ** -3.0, scalar2=EPS * C ** -2.0,
+                out=var_eps[:, a:b], in0=deviation[:, a:b], scalar1=C ** -3.0, scalar2=EPS * C ** -2.0,
                 op0=ALU.mult, op1=ALU.add,
             )
-            rstd = small("u_rstd")
-            nc.gpsimd.tensor_tensor(out=rstd[:], in0=var_eps[:], in1=neg_half[:, 0:1], op=ALU.pow)
-            v_stats[g, j] = (v_mean, rstd)
+            nc.gpsimd.tensor_tensor(out=rs[:, a:b], in0=var_eps[:, a:b], in1=neg_half[:, a:b], op=ALU.pow)
 
         def edge_plus_b_bn(g, j):
             bank = psum.tile([P, C], F32, tag="tp", name="residual")
@@ -360,7 +383,7 @@ def tile_comformerconvedgelayer_pb_t_kernel(
             v = v_rows[g]
             for j in tiles:
                 nc.vector.scalar_tensor_tensor(
-                    out=v[:, j, :], in0=v[:, j, :], scalar=v_stats[g, j][0][:], in1=g_bn_bc[:],
+                    out=v[:, j, :], in0=v[:, j, :], scalar=v_stats[g][2][:, j : j + 1], in1=g_bn_bc[:],
                     op0=ALU.subtract, op1=ALU.mult,
                 )
 
@@ -369,7 +392,7 @@ def tile_comformerconvedgelayer_pb_t_kernel(
             for j in tiles:
                 residual = edge_plus_b_bn(g, j)
                 nc.vector.scalar_tensor_tensor(
-                    out=v[:, j, :], in0=v[:, j, :], scalar=v_stats[g, j][1][:], in1=residual[:],
+                    out=v[:, j, :], in0=v[:, j, :], scalar=v_stats[g][4][:, j : j + 1], in1=residual[:],
                     op0=ALU.mult, op1=ALU.add,
                 )
 
@@ -448,15 +471,12 @@ def tile_comformerconvedgelayer_pb_t_kernel(
         for i in range(N_STEPS):
             gated = i - 1
             ended, age = divmod(i - (T + 1), T)
-            alpha_rows(i, LOW)
+            statistics(i, LOW)
             sigmoid(gated, LOW)
             quantise_hk(i + 1)
+            aggregate(i, LOW)
             gate_quantise(gated - 1)
             quantise_edge(i + 1)
-            if i == 0:
-                wm_grouped = group_weight(wm_raw, regroup)
-                quantise_hm(0)
-                wm = quantise_weight(wm_grouped, "wm")
             if i == 1:
                 wc = quantise_weight(wc_grouped, "wc")
                 bc_sum = sb.tile([P, C], F32)
@@ -465,37 +485,47 @@ def tile_comformerconvedgelayer_pb_t_kernel(
                 scale_deviation(ended, LOW)
             if ended >= 0 and age == 2:
                 scale_deviation(ended, HIGH)
-            normalise(i, LOW)
+            power(i, LOW)
             if starts_group(i + 1):
                 q_project((i + 1) // T)
             msg_project(gated, LOW)
             gate_multiply(gated, LOW)
-            alpha_rows(i, HIGH)
+            statistics(i, HIGH)
+            if i == 0:
+                wm_grouped = group_weight(wm_raw, regroup)
+                quantise_hm(0)
+                wm = quantise_weight(wm_grouped, "wm")
+                wc_grouped = group_weight(wc_raw, regroup)
+            shift(i, LOW)
+            aggregate(i, HIGH)
             sigmoid(gated, HIGH)
             quantise_hm(i + 1)
-            normalise(i, HIGH)
             msg_project(gated, HIGH)
+            power(i, HIGH)
             gate_multiply(gated, HIGH)
-            gate_regroup(gated, i < N_STEPS - 1)
-            if i == 0:
-                wc_grouped = group_weight(wc_raw, gpsimd_regroup)
+            shift(i, HIGH)
+            normalise(i, LOW)
+            k_project(i + 1, LOW)
+            transpose_edge(i + TRANSPOSE_AHEAD)
+            gate_regroup(gated, "G")
+            alpha(i + 1, LOW)
+            normalise(i, HIGH)
+            transpose_hk(i + TRANSPOSE_AHEAD)
+            k_project(i + 1, HIGH)
+            alpha(i + 1, HIGH)
+            transpose_hm(i + TRANSPOSE_AHEAD)
+            load_step(i + LOAD_AHEAD)
+            if ended >= 0 and age == 0:
+                for j in ALL:
+                    u_product(ended, j, range(T))
+                    u_statistics(ended, j)
+                u_rstd(ended, ALL)
             if ended >= 0 and age == 1:
                 add_edge(ended, LOW)
                 sigmoid_of_minus(ended, LOW)
             if ended >= 0 and age == 2:
                 add_edge(ended, HIGH)
                 sigmoid_of_minus(ended, HIGH)
-            if ended >= 0 and age == 0:
-                for j in ALL:
-                    u_product(ended, j, range(T))
-                    u_statistics(ended, j)
-            k_project(i + 1, LOW)
-            transpose_edge(i + TRANSPOSE_AHEAD)
-            transpose_hk(i + TRANSPOSE_AHEAD)
-            k_project(i + 1, HIGH)
-            transpose_hm(i + TRANSPOSE_AHEAD)
-            load_step(i + LOAD_AHEAD)
-            alpha(i + 1, ALL)
 
         last, g = N_STEPS - 1, N_GROUPS - 1
         scale_deviation(g - 1, HIGH)
@@ -505,7 +535,7 @@ def tile_comformerconvedgelayer_pb_t_kernel(
         sigmoid(last, ALL)
         sigmoid_of_minus(g - 1, HIGH)
         gate_multiply(last, ALL)
-        gate_regroup(last, False)
+        gate_regroup(last, "V")
         gate_quantise(last)
         logarithm(0, ALL)
         for j in ALL:
@@ -513,8 +543,11 @@ def tile_comformerconvedgelayer_pb_t_kernel(
         for j in ALL:
             u_product(g, j, [T - 1])
             u_statistics(g, j)
+            if j == 1:
+                u_rstd(g, LOW)
         logarithm(1, ALL)
         bring_back_sigmoid()
+        u_rstd(g, HIGH)
         scale_deviation(g, LOW)
         add_edge(g, LOW)
         scale_deviation(g, HIGH)

@@ -428,6 +428,10 @@ def tile_comformerconvedgelayer_pb_t_kernel(
             nc.sync.dma_start(
                 out=vec_rows[v * CT : (v + 1) * CT, :], in_=vec.rearrange("(t p) -> t p", p=P)
             )
+        hk_rows[0] = load_rows(hk_v[0][:, :, 0, :], "hk_rows", LOAD_AHEAD)
+        wk_raw = load_first_stage_weight(Wk2)
+        hm_rows[0] = load_rows(hm_v[0][:, :, 0, :], "hm_rows", LOAD_AHEAD)
+        transpose_edge(-1)
         cols_ps = psum.tile([P, P], BF16, tag="tp")
         nc.tensor.transpose(cols_ps[:], vec_rows[:], ident_bf16[:])
         cols = sb.tile([P, P], F32)
@@ -440,10 +444,6 @@ def tile_comformerconvedgelayer_pb_t_kernel(
         bq_scaled_col = sb.tile([P, CT], F32)
         nc.vector.tensor_scalar_mul(out=bq_scaled_col[:], in0=cols[:, 0:CT], scalar1=inv_sqrt_c)
 
-        hk_rows[0] = load_rows(hk_v[0][:, :, 0, :], "hk_rows", LOAD_AHEAD)
-        wk_raw = load_first_stage_weight(Wk2)
-        hm_rows[0] = load_rows(hm_v[0][:, :, 0, :], "hm_rows", LOAD_AHEAD)
-        transpose_edge(-1)
         wq_grouped = group_weight(wq_raw, regroup)
         quantise_edge(-1)
         wq = quantise_weight(wq_grouped, "wq")
@@ -463,10 +463,8 @@ def tile_comformerconvedgelayer_pb_t_kernel(
         nc.sync.dma_start(out=g_bn_bc[:], in_=g_bn.partition_broadcast(P))
         b_bn_bc = sb.tile([P, C], BF16)
         nc.sync.dma_start(out=b_bn_bc[:], in_=b_bn.partition_broadcast(P))
-        transpose_hm(0)
-        alpha(0, ALL)
         transpose_hk(1)
-        transpose_hm(1)
+        alpha(0, ALL)
 
         for i in range(N_STEPS):
             gated = i - 1
@@ -478,6 +476,9 @@ def tile_comformerconvedgelayer_pb_t_kernel(
             gate_quantise(gated - 1)
             quantise_edge(i + 1)
             if i == 1:
+                wm = quantise_weight(wm_grouped, "wm")
+                wc_grouped = group_weight(wc_raw, regroup)
+            if i == 2:
                 wc = quantise_weight(wc_grouped, "wc")
                 bc_sum = sb.tile([P, C], F32)
                 nc.vector.tensor_scalar_mul(out=bc_sum[:], in0=bc_bc[:], scalar1=float(T) / C)
@@ -492,14 +493,11 @@ def tile_comformerconvedgelayer_pb_t_kernel(
             gate_multiply(gated, LOW)
             statistics(i, HIGH)
             if i == 0:
-                wm_grouped = group_weight(wm_raw, regroup)
-                quantise_hm(0)
-                wm = quantise_weight(wm_grouped, "wm")
-                wc_grouped = group_weight(wc_raw, regroup)
+                transpose_hm(0)
             shift(i, LOW)
             aggregate(i, HIGH)
             sigmoid(gated, HIGH)
-            quantise_hm(i + 1)
+            quantise_hm(i)
             msg_project(gated, HIGH)
             power(i, HIGH)
             gate_multiply(gated, HIGH)
@@ -507,13 +505,15 @@ def tile_comformerconvedgelayer_pb_t_kernel(
             normalise(i, LOW)
             k_project(i + 1, LOW)
             transpose_edge(i + TRANSPOSE_AHEAD)
-            gate_regroup(gated, "G")
+            gate_regroup(gated, "G" if i < N_STEPS - 1 else "V")
             alpha(i + 1, LOW)
             normalise(i, HIGH)
             transpose_hk(i + TRANSPOSE_AHEAD)
             k_project(i + 1, HIGH)
             alpha(i + 1, HIGH)
-            transpose_hm(i + TRANSPOSE_AHEAD)
+            if i == 0:
+                wm_grouped = group_weight(wm_raw, regroup)
+            transpose_hm(i + 1)
             load_step(i + LOAD_AHEAD)
             if ended >= 0 and age == 0:
                 for j in ALL:
@@ -528,12 +528,10 @@ def tile_comformerconvedgelayer_pb_t_kernel(
                 sigmoid_of_minus(ended, HIGH)
 
         last, g = N_STEPS - 1, N_GROUPS - 1
-        scale_deviation(g - 1, HIGH)
-        add_edge(g - 1, HIGH)
         gate_quantise(last - 1)
+        scale_deviation(g - 1, HIGH)
         msg_project(last, ALL)
         sigmoid(last, ALL)
-        sigmoid_of_minus(g - 1, HIGH)
         gate_multiply(last, ALL)
         gate_regroup(last, "V")
         gate_quantise(last)
@@ -545,15 +543,17 @@ def tile_comformerconvedgelayer_pb_t_kernel(
             u_statistics(g, j)
             if j == 1:
                 u_rstd(g, LOW)
-        logarithm(1, ALL)
         bring_back_sigmoid()
         u_rstd(g, HIGH)
+        add_edge(g - 1, HIGH)
+        sigmoid_of_minus(g - 1, HIGH)
         scale_deviation(g, LOW)
         add_edge(g, LOW)
         scale_deviation(g, HIGH)
         add_edge(g, HIGH)
         sigmoid_of_minus(g, ALL)
         store(0, ALL)
+        logarithm(1, ALL)
         store(1, ALL)
         logarithm(g, ALL)
         store(g, ALL)

@@ -37,7 +37,7 @@ def tile_comformerconvedgelayer_pb_t_kernel(
     nc = tc.nc
     with ExitStack() as ctx:
         sb = ctx.enter_context(tc.tile_pool(name="sb", bufs=1))
-        psum = ctx.enter_context(tc.psum_pool(name="psum", bufs=4))
+        psum = ctx.enter_context(tc.psum_pool(name="psum", bufs=8))
         ctx.enter_context(tc.manual_schedule())
 
         def matmul_mx(acc, stationary, moving, start=True, stop=True):
@@ -78,7 +78,7 @@ def tile_comformerconvedgelayer_pb_t_kernel(
         def transposed_product(weight, moving):
             banks = []
             for ct in range(CT):
-                acc = psum.tile([P, GROUP], F32, tag="mx", name="acc")
+                acc = psum.tile([P, GROUP], F32, tag="bank", name="acc")
                 matmul_mx(acc[:], columns(weight, ct), whole(moving))
                 banks.append(acc)
             return banks
@@ -128,7 +128,7 @@ def tile_comformerconvedgelayer_pb_t_kernel(
         hk_rows, hk_grouped, hk_q, k_banks = {}, {}, {}, {}
         hm_rows, hm_grouped, hm_q, msg_banks = {}, {}, {}, {}
         alpha_t, rows_t, gate_t, gated_q = {}, {}, {}, {}
-        gated_t, gated_grouped, alpha_bn, alpha_stats = {}, {}, {}, {}
+        gated_t, gated_grouped, alpha_bn, alpha_banks, alpha_stats = {}, {}, {}, {}, {}
         v_rows, v_stats, softplus, u_banks = {}, {}, {}, {}
 
         def load_rows(view, tag, bufs):
@@ -154,7 +154,7 @@ def tile_comformerconvedgelayer_pb_t_kernel(
             grouped = sb.tile([P, PACK * GROUP], BF16, tag="x_grouped", bufs=4, align_bytes=64)
             grouped_words = grouped[:].bitcast(F32).rearrange("p (n u) -> p n u", u=2)
             for half in range(2):
-                bank = psum.tile([P, 2, 2 * P], F32, tag="tp")
+                bank = psum.tile([P, 2, 2 * P], F32, tag="bank")
                 for jj in range(2):
                     words = rows[:, 2 * half + jj, :].bitcast(F32)
                     for u in range(2):
@@ -204,7 +204,7 @@ def tile_comformerconvedgelayer_pb_t_kernel(
 
         def product(banks, s, weight, moving, cts):
             for ct in cts:
-                banks[s, ct] = psum.tile([P, GROUP], F32, tag="mx", name="acc")
+                banks[s, ct] = psum.tile([P, GROUP], F32, tag="bank", name="acc")
                 matmul_mx(banks[s, ct][:], columns(weight, ct), whole(moving))
 
         def k_project(s, cts):
@@ -223,7 +223,7 @@ def tile_comformerconvedgelayer_pb_t_kernel(
                 )
 
         def alpha_rows(s, j):
-            bank = psum.tile([P, C], F32, tag="tp", name="alpha_bank")
+            bank = psum.tile([P, C], F32, tag="bank", name="alpha_bank")
             for ct in range(CT):
                 nc.tensor.transpose(
                     bank[:, ct * P : (ct + 1) * P],
@@ -238,7 +238,8 @@ def tile_comformerconvedgelayer_pb_t_kernel(
             if 0 in tiles:
                 alpha_bn[s] = sb.tile([P, J, 6], F32, tag="alpha_bn", bufs=2, name="alpha_bn")
             for j in tiles:
-                nc.vector.bn_stats(out=alpha_bn[s][:, j, :], in_=alpha_rows(s, j)[:])
+                alpha_banks[s, j] = alpha_rows(s, j)
+                nc.vector.bn_stats(out=alpha_bn[s][:, j, :], in_=alpha_banks[s, j][:])
 
         def aggregate(s, tiles):
             if not is_step(s):
@@ -276,7 +277,7 @@ def tile_comformerconvedgelayer_pb_t_kernel(
             for j in tiles:
                 mean_var, var_eps, rs, sh = alpha_stats[s]
                 nc.scalar.activation(
-                    out=rows_t[s][:, j, :], in_=alpha_rows(s, j)[:], func=ACT.Identity,
+                    out=rows_t[s][:, j, :], in_=alpha_banks[s, j][:], func=ACT.Identity,
                     bias=sh[:, j : j + 1], scale=rs[:, j : j + 1],
                 )
 
@@ -286,7 +287,7 @@ def tile_comformerconvedgelayer_pb_t_kernel(
             if 0 in cts:
                 gate_t[s] = sb.tile([P, CT, GROUP], F32, tag="gate_t", bufs=1, name="gate_t")
             for ct in cts:
-                bank = psum.tile([P, GROUP], F32, tag="tp")
+                bank = psum.tile([P, GROUP], F32, tag="bank")
                 for j in range(J):
                     nc.tensor.transpose(
                         bank[:, j * P : (j + 1) * P],
@@ -335,7 +336,7 @@ def tile_comformerconvedgelayer_pb_t_kernel(
 
         def u_product(g, j, directions):
             if 0 in directions:
-                u_banks[g, j] = psum.tile([P, C], F32, tag="mx", name="u_bank")
+                u_banks[g, j] = psum.tile([P, C], F32, tag="bank", name="u_bank")
             for t in directions:
                 matmul_mx(
                     u_banks[g, j][:], columns(gated_q[T * g + t], j), whole(wc),
@@ -374,7 +375,7 @@ def tile_comformerconvedgelayer_pb_t_kernel(
             nc.gpsimd.tensor_tensor(out=rs[:, a:b], in0=var_eps[:, a:b], in1=neg_half[:, a:b], op=ALU.pow)
 
         def edge_plus_b_bn(g, j):
-            bank = psum.tile([P, C], F32, tag="tp", name="residual")
+            bank = psum.tile([P, C], F32, tag="bank", name="residual")
             nc.tensor.matmul(bank[:], ident_bf16[:], edge_rows[g][:, j, :], start=True, stop=False)
             nc.tensor.matmul(bank[:], ident_bf16[:], b_bn_bc[:], start=False, stop=True)
             return bank
@@ -420,6 +421,7 @@ def tile_comformerconvedgelayer_pb_t_kernel(
                 nc.sync.dma_start(out=out_v[g][:, j, :], in_=softplus[g][:, j, :])
 
         ALL, LOW, HIGH = range(J), (0, 1), (2, 3)
+        bring_back_sigmoid()
         load_step(-1)
         wq_raw = load_first_stage_weight(Wq)
         vec_rows = sb.tile([P, P], BF16)
@@ -432,7 +434,7 @@ def tile_comformerconvedgelayer_pb_t_kernel(
         wk_raw = load_first_stage_weight(Wk2)
         hm_rows[0] = load_rows(hm_v[0][:, :, 0, :], "hm_rows", LOAD_AHEAD)
         transpose_edge(-1)
-        cols_ps = psum.tile([P, P], BF16, tag="tp")
+        cols_ps = psum.tile([P, P], BF16, tag="bank")
         nc.tensor.transpose(cols_ps[:], vec_rows[:], ident_bf16[:])
         cols = sb.tile([P, P], F32)
         nc.vector.tensor_copy(out=cols[:], in_=cols_ps[:])
@@ -502,14 +504,14 @@ def tile_comformerconvedgelayer_pb_t_kernel(
             power(i, HIGH)
             gate_multiply(gated, HIGH)
             shift(i, HIGH)
-            normalise(i, LOW)
             k_project(i + 1, LOW)
+            k_project(i + 1, HIGH)
+            normalise(i, LOW)
             transpose_edge(i + TRANSPOSE_AHEAD)
             gate_regroup(gated, "G" if i < N_STEPS - 1 else "V")
             alpha(i + 1, LOW)
-            normalise(i, HIGH)
             transpose_hk(i + TRANSPOSE_AHEAD)
-            k_project(i + 1, HIGH)
+            normalise(i, HIGH)
             alpha(i + 1, HIGH)
             if i == 0:
                 wm_grouped = group_weight(wm_raw, regroup)

@@ -236,10 +236,10 @@ def tile_comformerconvedgelayer_pb_t_kernel(
             if not is_step(s):
                 return
             if 0 in tiles:
-                alpha_bn[s] = sb.tile([P, J, 6], F32, tag="alpha_bn", bufs=2, name="alpha_bn")
+                alpha_bn[s] = bn_tuples[s % 2]
             for j in tiles:
                 alpha_banks[s, j] = alpha_rows(s, j)
-                nc.vector.bn_stats(out=alpha_bn[s][:, j, :], in_=alpha_banks[s, j][:])
+                nc.vector.bn_stats(out=alpha_bn[s][:, j, 0:6], in_=alpha_banks[s, j][:])
 
         def aggregate(s, tiles):
             if not is_step(s):
@@ -247,7 +247,7 @@ def tile_comformerconvedgelayer_pb_t_kernel(
             if 0 in tiles:
                 alpha_stats[s] = tuple(
                     sb.tile([P, J] + more, F32, tag="alpha_" + tag, bufs=2, name=tag)
-                    for tag, more in (("mean_var", [2]), ("var_eps", []), ("rstd", []), ("shift", []))
+                    for tag, more in (("mean_var", [2]), ("rstd", []), ("shift", []))
                 )
             for j in tiles:
                 nc.vector.bn_aggr(out=alpha_stats[s][0][:, j, :], in_=alpha_bn[s][:, j, :])
@@ -255,15 +255,14 @@ def tile_comformerconvedgelayer_pb_t_kernel(
         def power(s, tiles):
             if not is_step(s):
                 return
-            mean_var, var_eps, rs, sh = alpha_stats[s]
+            mean_var, rs, sh = alpha_stats[s]
             a, b = tiles[0], tiles[-1] + 1
-            nc.vector.tensor_scalar_add(out=var_eps[:, a:b], in0=mean_var[:, a:b, 1], scalar1=EPS)
-            nc.gpsimd.tensor_tensor(out=rs[:, a:b], in0=var_eps[:, a:b], in1=neg_half[:, a:b], op=ALU.pow)
+            nc.gpsimd.tensor_tensor(out=rs[:, a:b], in0=mean_var[:, a:b, 1], in1=neg_half[:, a:b], op=ALU.pow)
 
         def shift(s, tiles):
             if not is_step(s):
                 return
-            mean_var, var_eps, rs, sh = alpha_stats[s]
+            mean_var, rs, sh = alpha_stats[s]
             a, b = tiles[0], tiles[-1] + 1
             nc.vector.scalar_tensor_tensor(
                 out=sh[:, a:b], in0=mean_var[:, a:b, 0], scalar=-1.0, in1=rs[:, a:b], op0=ALU.mult, op1=ALU.mult
@@ -275,7 +274,7 @@ def tile_comformerconvedgelayer_pb_t_kernel(
             if 0 in tiles:
                 rows_t[s] = sb.tile([P, J, C], F32, tag="rows_t", bufs=1, name="rows_t")
             for j in tiles:
-                mean_var, var_eps, rs, sh = alpha_stats[s]
+                mean_var, rs, sh = alpha_stats[s]
                 nc.scalar.activation(
                     out=rows_t[s][:, j, :], in_=alpha_banks[s, j][:], func=ACT.Identity,
                     bias=sh[:, j : j + 1], scale=rs[:, j : j + 1],
@@ -421,6 +420,12 @@ def tile_comformerconvedgelayer_pb_t_kernel(
                 nc.sync.dma_start(out=out_v[g][:, j, :], in_=softplus[g][:, j, :])
 
         ALL, LOW, HIGH = range(J), (0, 1), (2, 3)
+        bn_tuples = []
+        for x in range(2):
+            tuples = sb.tile([P, J, 9], F32, name="bn_tuples%d" % x)
+            nc.vector.memset(tuples[:], 0.0)
+            nc.vector.tensor_scalar_add(out=tuples[:, :, 8], in0=tuples[:, :, 7], scalar1=C * EPS)
+            bn_tuples.append(tuples)
         bring_back_sigmoid()
         load_step(-1)
         wq_raw = load_first_stage_weight(Wq)

@@ -22,11 +22,10 @@ CT = C // P
 N_STEPS = N_GROUPS * T
 EPS = 1e-5
 RUN = 4
-STAT_BUFS = 3 * J
+FLOOR = 2.0 ** -60
 
 LOAD_AHEAD = 3
 TRANSPOSE_AHEAD = 2
-GROUP_END_BUFS = 3
 
 FLOPS = 2 * C * C * (E + 3 * E * T)
 
@@ -63,28 +62,17 @@ def tile_comformerconvedgelayer_pb_t_kernel(
             nc.vector.quantize_mx(out=codes[:].bitcast(FP8X4), scales=scales[:], in_=grouped)
             return codes, scales
 
-        def gpsimd_regroup(grouped, planes):
-            nc.gpsimd.tensor_scalar(
-                out=grouped[:], in0=planes[:].rearrange("p t n -> p n t"),
-                scalar1=1.0, scalar2=0.0, op0=ALU.mult, op1=ALU.add,
-            )
-
         def regroup(grouped, planes):
             nc.vector.tensor_copy(
                 out=grouped[:].rearrange("p (c i) t -> p c t i", i=RUN),
                 in_=planes[:].rearrange("p t (c i) -> p c t i", i=RUN),
             )
 
-        def transposed_product(weight, moving):
-            banks = []
-            for ct in range(CT):
-                acc = psum.tile([P, GROUP], F32, tag="bank", name="acc")
-                matmul_mx(acc[:], columns(weight, ct), whole(moving))
-                banks.append(acc)
-            return banks
-
-        def small(tag):
-            return sb.tile([P, 1], F32, tag=tag, bufs=STAT_BUFS, name=tag)
+        def gpsimd_regroup(grouped, planes):
+            nc.gpsimd.tensor_scalar(
+                out=grouped[:], in0=planes[:].rearrange("p t n -> p n t"),
+                scalar1=1.0, scalar2=0.0, op0=ALU.mult, op1=ALU.add,
+            )
 
         ident_f32 = sb.tile([P, P], F32)
         make_identity(nc, ident_f32[:])
@@ -94,7 +82,7 @@ def tile_comformerconvedgelayer_pb_t_kernel(
         nc.vector.memset(neg_half[:], -0.5)
         table_warmer = sb.tile([P, 1], F32)
         floor = sb.tile([P, 1], F32)
-        nc.vector.memset(floor[:], 2.0 ** -60)
+        nc.vector.memset(floor[:], FLOOR)
 
         def load_weight(w_view, split):
             raw = sb.tile([P, PACK, C], BF16, tag="w_raw", bufs=2)
@@ -124,11 +112,12 @@ def tile_comformerconvedgelayer_pb_t_kernel(
         hm_v = h_m.rearrange("(g p j) t c -> g p j t c", g=N_GROUPS, p=P)
         out_v = out.rearrange("(g p j) c -> g p j c", g=N_GROUPS, p=P)
 
-        edge_rows, edge_grouped, edge_q, q_t = {}, {}, {}, {}
+        edge_rows, edge_grouped, edge_q, q_banks, q_t = {}, {}, {}, {}, {}
         hk_rows, hk_grouped, hk_q, k_banks = {}, {}, {}, {}
         hm_rows, hm_grouped, hm_q, msg_banks = {}, {}, {}, {}
-        alpha_t, rows_t, gate_t, gated_q = {}, {}, {}, {}
-        gated_t, gated_grouped, alpha_bn, alpha_banks, alpha_stats = {}, {}, {}, {}, {}
+        alpha_t, alpha_banks, normed, gate_t = {}, {}, {}, {}
+        mean_var, rstd, shift, last = {}, {}, {}, {}
+        gated_t, gated_grouped, gated_q = {}, {}, {}
         v_rows, v_stats, softplus, u_banks = {}, {}, {}, {}
 
         def load_rows(view, tag, bufs):
@@ -193,19 +182,19 @@ def tile_comformerconvedgelayer_pb_t_kernel(
             if is_step(s):
                 hm_q[s] = quantise(hm_grouped[s][:], GROUP, "hm", 3)
 
+        def product(banks, key, weight, moving, cts):
+            for ct in cts:
+                banks[key, ct] = psum.tile([P, GROUP], F32, tag="bank", name="acc")
+                matmul_mx(banks[key, ct][:], columns(weight, ct), whole(moving))
+
         def q_project(g):
-            banks = transposed_product(wq, edge_q[g])
+            product(q_banks, g, wq, edge_q[g], ALL)
             q_t[g] = sb.tile([P, CT, GROUP], F32, tag="q_t", bufs=2, name="q_t")
-            for ct in range(CT):
+            for ct in ALL:
                 nc.scalar.activation(
-                    out=q_t[g][:, ct, :], in_=banks[ct][:], func=ACT.Identity,
+                    out=q_t[g][:, ct, :], in_=q_banks[g, ct][:], func=ACT.Identity,
                     bias=bq_scaled_col[:, ct : ct + 1], scale=inv_sqrt_c,
                 )
-
-        def product(banks, s, weight, moving, cts):
-            for ct in cts:
-                banks[s, ct] = psum.tile([P, GROUP], F32, tag="bank", name="acc")
-                matmul_mx(banks[s, ct][:], columns(weight, ct), whole(moving))
 
         def k_project(s, cts):
             if is_step(s):
@@ -230,54 +219,85 @@ def tile_comformerconvedgelayer_pb_t_kernel(
                     alpha_t[s][:, ct, j * P : (j + 1) * P],
                     ident_f32[:],
                 )
+            alpha_banks[s, j] = bank
             return bank
 
         def statistics(s, tiles):
-            if not is_step(s):
-                return
-            if 0 in tiles:
-                alpha_bn[s] = bn_tuples[s % 2]
-            for j in tiles:
-                alpha_banks[s, j] = alpha_rows(s, j)
-                nc.vector.bn_stats(out=alpha_bn[s][:, j, 0:6], in_=alpha_banks[s, j][:])
+            if is_step(s):
+                for j in tiles:
+                    bank = alpha_rows(s, j)
+                    nc.vector.bn_stats(out=bn_triples[s % 2][:, j, 0:6], in_=bank[:])
 
         def aggregate(s, tiles):
             if not is_step(s):
                 return
             if 0 in tiles:
-                alpha_stats[s] = tuple(
-                    sb.tile([P, J] + more, F32, tag="alpha_" + tag, bufs=2, name=tag)
-                    for tag, more in (("mean_var", [2]), ("rstd", []), ("shift", []))
-                )
+                mean_var[s] = sb.tile([P, J, 2], F32, tag="alpha_mean_var", bufs=2, name="mean_var")
+                rstd[s] = sb.tile([P, J], F32, tag="alpha_rstd", bufs=2, name="rstd")
+                shift[s] = sb.tile([P, J], F32, tag="alpha_shift", bufs=2, name="shift")
             for j in tiles:
-                nc.vector.bn_aggr(out=alpha_stats[s][0][:, j, :], in_=alpha_bn[s][:, j, :])
+                nc.vector.bn_aggr(out=mean_var[s][:, j, :], in_=bn_triples[s % 2][:, j, :])
 
         def power(s, tiles):
-            if not is_step(s):
-                return
-            mean_var, rs, sh = alpha_stats[s]
-            a, b = tiles[0], tiles[-1] + 1
-            nc.gpsimd.tensor_tensor(out=rs[:, a:b], in0=mean_var[:, a:b, 1], in1=neg_half[:, a:b], op=ALU.pow)
+            if is_step(s):
+                a, b = tiles[0], tiles[-1] + 1
+                nc.gpsimd.tensor_tensor(
+                    out=rstd[s][:, a:b], in0=mean_var[s][:, a:b, 1], in1=neg_half[:, a:b], op=ALU.pow
+                )
 
-        def shift(s, tiles):
+        def shift_of(s, tiles):
+            if is_step(s):
+                a, b = tiles[0], tiles[-1] + 1
+                nc.vector.scalar_tensor_tensor(
+                    out=shift[s][:, a:b], in0=mean_var[s][:, a:b, 0], scalar=-1.0, in1=rstd[s][:, a:b],
+                    op0=ALU.mult, op1=ALU.mult,
+                )
+
+        def last_mean(s):
             if not is_step(s):
                 return
-            mean_var, rs, sh = alpha_stats[s]
-            a, b = tiles[0], tiles[-1] + 1
-            nc.vector.scalar_tensor_tensor(
-                out=sh[:, a:b], in0=mean_var[:, a:b, 0], scalar=-1.0, in1=rs[:, a:b], op0=ALU.mult, op1=ALU.mult
+            bank = alpha_rows(s, 3)
+            last[s] = tuple(
+                sb.tile([P, 1], F32, tag="last_" + tag, bufs=2, name=tag)
+                for tag in ("neg_mean", "deviation", "var_eps", "rstd", "shift")
             )
+            neg_mean = last[s][0]
+            unused = sb.tile([P, C], BF16, tag="unused", bufs=1)
+            nc.scalar.activation(
+                out=unused[:], in_=bank[:], func=ACT.Identity, scale=-1.0 / C, accum_out=neg_mean[:]
+            )
+
+        def last_deviation(s):
+            if is_step(s):
+                neg_mean, deviation = last[s][0:2]
+                unused = sb.tile([P, C], BF16, tag="unused", bufs=1)
+                nc.scalar.activation(
+                    out=unused[:], in_=alpha_banks[s, 3][:], func=ACT.Square, bias=neg_mean[:],
+                    accum_out=deviation[:],
+                )
+
+        def last_power(s):
+            if is_step(s):
+                neg_mean, deviation, var_eps, last_rstd, last_shift = last[s]
+                nc.gpsimd.tensor_scalar(
+                    out=var_eps[:], in0=deviation[:], scalar1=1.0 / C, scalar2=EPS,
+                    op0=ALU.mult, op1=ALU.add,
+                )
+                nc.gpsimd.tensor_tensor(out=last_rstd[:], in0=var_eps[:], in1=neg_half[:, 0:1], op=ALU.pow)
+                nc.gpsimd.tensor_tensor(out=last_shift[:], in0=neg_mean[:], in1=last_rstd[:], op=ALU.mult)
 
         def normalise(s, tiles):
             if not is_step(s):
                 return
             if 0 in tiles:
-                rows_t[s] = sb.tile([P, J, C], F32, tag="rows_t", bufs=1, name="rows_t")
+                normed[s] = sb.tile([P, J, C], F32, tag="normed", bufs=1, name="normed")
             for j in tiles:
-                mean_var, rs, sh = alpha_stats[s]
+                scale, bias = rstd[s][:, j : j + 1], shift[s][:, j : j + 1]
+                if j == 3:
+                    scale, bias = last[s][3][:], last[s][4][:]
                 nc.scalar.activation(
-                    out=rows_t[s][:, j, :], in_=alpha_banks[s, j][:], func=ACT.Identity,
-                    bias=sh[:, j : j + 1], scale=rs[:, j : j + 1],
+                    out=normed[s][:, j, :], in_=alpha_banks[s, j][:], func=ACT.Identity,
+                    bias=bias, scale=scale,
                 )
 
         def sigmoid(s, cts):
@@ -290,7 +310,7 @@ def tile_comformerconvedgelayer_pb_t_kernel(
                 for j in range(J):
                     nc.tensor.transpose(
                         bank[:, j * P : (j + 1) * P],
-                        rows_t[s][:, j, ct * P : (ct + 1) * P],
+                        normed[s][:, j, ct * P : (ct + 1) * P],
                         ident_f32[:],
                     )
                 nc.scalar.activation(
@@ -313,21 +333,13 @@ def tile_comformerconvedgelayer_pb_t_kernel(
                     in1=gate_t[s][:, ct, :], op0=ALU.add, op1=ALU.mult,
                 )
 
-        def gate_regroup(s, engine):
+        def gate_regroup(s, copy):
             if not is_step(s):
                 return
             gated_grouped[s] = sb.tile(
                 [P, GROUP, PACK], BF16, tag="gated_grouped", bufs=2, align_bytes=64, name="gated_grouped"
             )
-            if engine == "G":
-                gpsimd_regroup(gated_grouped[s], gated_t[s])
-            elif engine == "S":
-                nc.scalar.copy(
-                    out=gated_grouped[s][:].rearrange("p (c i) t -> p c t i", i=RUN),
-                    in_=gated_t[s][:].rearrange("p t (c i) -> p c t i", i=RUN),
-                )
-            else:
-                regroup(gated_grouped[s], gated_t[s])
+            copy(gated_grouped[s], gated_t[s])
 
         def gate_quantise(s):
             if is_step(s):
@@ -344,14 +356,14 @@ def tile_comformerconvedgelayer_pb_t_kernel(
 
         def u_statistics(g, j):
             if j == 0:
-                v_rows[g] = sb.tile([P, J, C], F32, tag="v_rows", bufs=GROUP_END_BUFS, name="v_rows")
-                softplus[g] = sb.tile([P, J, C], F32, tag="softplus", bufs=GROUP_END_BUFS, name="softplus")
+                v_rows[g] = sb.tile([P, J, C], F32, tag="v_rows", bufs=N_GROUPS, name="v_rows")
+                softplus[g] = sb.tile([P, J, C], F32, tag="softplus", bufs=N_GROUPS, name="softplus")
                 v_stats[g] = tuple(
                     sb.tile([P, J], F32, tag="u_" + tag, bufs=2, name=tag)
                     for tag in ("mean", "deviation", "v_mean", "var_eps", "rstd")
                 )
             v = v_rows[g]
-            mean, deviation, v_mean, var_eps, rs = v_stats[g]
+            mean, deviation, v_mean, var_eps, v_rstd = v_stats[g]
             nc.vector.scalar_tensor_tensor(
                 out=v[:, j, :], in0=u_banks[g, j][:], scalar=1.0 / C, in1=bc_sum[:],
                 op0=ALU.mult, op1=ALU.add, accum_out=mean[:, j : j + 1],
@@ -362,7 +374,7 @@ def tile_comformerconvedgelayer_pb_t_kernel(
             )
 
         def u_rstd(g, tiles):
-            mean, deviation, v_mean, var_eps, rs = v_stats[g]
+            mean, deviation, v_mean, var_eps, v_rstd = v_stats[g]
             a, b = tiles[0], tiles[-1] + 1
             nc.gpsimd.tensor_scalar(
                 out=v_mean[:, a:b], in0=mean[:, a:b], scalar1=1.0 / C, scalar2=0.0, op0=ALU.mult, op1=ALU.add
@@ -371,7 +383,7 @@ def tile_comformerconvedgelayer_pb_t_kernel(
                 out=var_eps[:, a:b], in0=deviation[:, a:b], scalar1=C ** -3.0, scalar2=EPS * C ** -2.0,
                 op0=ALU.mult, op1=ALU.add,
             )
-            nc.gpsimd.tensor_tensor(out=rs[:, a:b], in0=var_eps[:, a:b], in1=neg_half[:, a:b], op=ALU.pow)
+            nc.gpsimd.tensor_tensor(out=v_rstd[:, a:b], in0=var_eps[:, a:b], in1=neg_half[:, a:b], op=ALU.pow)
 
         def edge_plus_b_bn(g, j):
             bank = psum.tile([P, C], F32, tag="bank", name="residual")
@@ -380,19 +392,19 @@ def tile_comformerconvedgelayer_pb_t_kernel(
             return bank
 
         def scale_deviation(g, tiles):
-            v = v_rows[g]
+            v, v_mean = v_rows[g], v_stats[g][2]
             for j in tiles:
                 nc.vector.scalar_tensor_tensor(
-                    out=v[:, j, :], in0=v[:, j, :], scalar=v_stats[g][2][:, j : j + 1], in1=g_bn_bc[:],
+                    out=v[:, j, :], in0=v[:, j, :], scalar=v_mean[:, j : j + 1], in1=g_bn_bc[:],
                     op0=ALU.subtract, op1=ALU.mult,
                 )
 
         def add_edge(g, tiles):
-            v = v_rows[g]
+            v, v_rstd = v_rows[g], v_stats[g][4]
             for j in tiles:
                 residual = edge_plus_b_bn(g, j)
                 nc.vector.scalar_tensor_tensor(
-                    out=v[:, j, :], in0=v[:, j, :], scalar=v_stats[g][4][:, j : j + 1], in1=residual[:],
+                    out=v[:, j, :], in0=v[:, j, :], scalar=v_rstd[:, j : j + 1], in1=residual[:],
                     op0=ALU.mult, op1=ALU.add,
                 )
 
@@ -408,7 +420,7 @@ def tile_comformerconvedgelayer_pb_t_kernel(
                     out=softplus[g][:, j, :], in_=softplus[g][:, j, :], func=ACT.Ln, bias=floor[:]
                 )
 
-        def bring_back_sigmoid():
+        def load_sigmoid_table():
             nc.scalar.activation(out=table_warmer[:], in_=neg_half[:, 0:1], func=ACT.Sigmoid)
 
         def store(g, tiles):
@@ -420,13 +432,13 @@ def tile_comformerconvedgelayer_pb_t_kernel(
                 nc.sync.dma_start(out=out_v[g][:, j, :], in_=softplus[g][:, j, :])
 
         ALL, LOW, HIGH = range(J), (0, 1), (2, 3)
-        bn_tuples = []
+        bn_triples = []
         for x in range(2):
-            tuples = sb.tile([P, J, 9], F32, name="bn_tuples%d" % x)
-            nc.vector.memset(tuples[:], 0.0)
-            nc.vector.tensor_scalar_add(out=tuples[:, :, 8], in0=tuples[:, :, 7], scalar1=C * EPS)
-            bn_tuples.append(tuples)
-        bring_back_sigmoid()
+            triples = sb.tile([P, J, 9], F32, name="bn_triples%d" % x)
+            nc.vector.memset(triples[:], 0.0)
+            nc.vector.tensor_scalar_add(out=triples[:, :, 8], in0=triples[:, :, 7], scalar1=C * EPS)
+            bn_triples.append(triples)
+        load_sigmoid_table()
         load_step(-1)
         wq_raw = load_first_stage_weight(Wq)
         vec_rows = sb.tile([P, P], BF16)
@@ -498,22 +510,26 @@ def tile_comformerconvedgelayer_pb_t_kernel(
                 q_project((i + 1) // T)
             msg_project(gated, LOW)
             gate_multiply(gated, LOW)
-            statistics(i, HIGH)
+            statistics(i, (2,))
+            last_mean(i)
             if i == 0:
                 transpose_hm(0)
-            shift(i, LOW)
-            aggregate(i, HIGH)
+            shift_of(i, LOW)
+            aggregate(i, (2,))
             sigmoid(gated, HIGH)
+            last_deviation(i)
             quantise_hm(i)
             msg_project(gated, HIGH)
-            power(i, HIGH)
+            power(i, (2,))
+            last_power(i)
             gate_multiply(gated, HIGH)
-            shift(i, HIGH)
+            shift_of(i, (2,))
             k_project(i + 1, LOW)
             k_project(i + 1, HIGH)
             normalise(i, LOW)
-            transpose_edge(i + TRANSPOSE_AHEAD)
-            gate_regroup(gated, "G" if i < N_STEPS - 1 else "V")
+            if i == 0:
+                transpose_edge(i + TRANSPOSE_AHEAD)
+            gate_regroup(gated, gpsimd_regroup if i < N_STEPS - 1 else regroup)
             alpha(i + 1, LOW)
             transpose_hk(i + TRANSPOSE_AHEAD)
             normalise(i, HIGH)
@@ -521,6 +537,8 @@ def tile_comformerconvedgelayer_pb_t_kernel(
             if i == 0:
                 wm_grouped = group_weight(wm_raw, regroup)
             transpose_hm(i + 1)
+            if i > 0:
+                transpose_edge(i + TRANSPOSE_AHEAD)
             load_step(i + LOAD_AHEAD)
             if ended >= 0 and age == 0:
                 for j in ALL:
@@ -534,14 +552,14 @@ def tile_comformerconvedgelayer_pb_t_kernel(
                 add_edge(ended, HIGH)
                 sigmoid_of_minus(ended, HIGH)
 
-        last, g = N_STEPS - 1, N_GROUPS - 1
-        gate_quantise(last - 1)
+        s, g = N_STEPS - 1, N_GROUPS - 1
+        gate_quantise(s - 1)
         scale_deviation(g - 1, HIGH)
-        msg_project(last, ALL)
-        sigmoid(last, ALL)
-        gate_multiply(last, ALL)
-        gate_regroup(last, "V")
-        gate_quantise(last)
+        msg_project(s, ALL)
+        sigmoid(s, ALL)
+        gate_multiply(s, ALL)
+        gate_regroup(s, regroup)
+        gate_quantise(s)
         logarithm(0, ALL)
         for j in ALL:
             u_product(g, j, range(T - 1))
@@ -550,7 +568,7 @@ def tile_comformerconvedgelayer_pb_t_kernel(
             u_statistics(g, j)
             if j == 1:
                 u_rstd(g, LOW)
-        bring_back_sigmoid()
+        load_sigmoid_table()
         u_rstd(g, HIGH)
         add_edge(g - 1, HIGH)
         sigmoid_of_minus(g - 1, HIGH)

import math
from contextlib import ExitStack

import concourse.mybir as mybir
from concourse.masks import make_identity

F32 = mybir.dt.float32
BF16 = mybir.dt.bfloat16
U32 = mybir.dt.uint32
U8 = mybir.dt.uint8
FP8X4 = mybir.dt.float8_e4m3fn_x4
ALU = mybir.AluOpType
ACT = mybir.ActivationFunctionType

P = 128
PACK = 4
E, T, C = 1536, 3, 512
GROUP = 512
N_GROUPS = E // GROUP
J = GROUP // P
CT = C // P
N_STEPS = N_GROUPS * T
EPS = 1e-5
RUN = 4
FLOOR = 2.0 ** -60

LOAD_AHEAD = 3
TRANSPOSE_AHEAD = 2

FLOPS = 2 * C * C * (E + 3 * E * T)


def tile_comformerconvedgelayer_pb_t_kernel(
    tc, edge, h_k, h_m, Wq, bq, Wk2, bk2, Wm2, bm2, Wc, bc, g_att, b_att, g_bn, b_bn, out
):
    nc = tc.nc
    with ExitStack() as ctx:
        sb = ctx.enter_context(tc.tile_pool(name="sb", bufs=1))
        psum = ctx.enter_context(tc.psum_pool(name="psum", bufs=8))
        ctx.enter_context(tc.manual_schedule())

        def matmul_mx(acc, stationary, moving, start=True, stop=True):
            nc.tensor.matmul_mx(
                out=acc,
                lhsT=stationary[0].bitcast(FP8X4),
                lhsT_scale=stationary[1],
                rhs=moving[0].bitcast(FP8X4),
                rhs_scale=moving[1],
                start=start,
                stop=stop,
            )

        def columns(operand, i):
            return operand[0][:, i * P : (i + 1) * P], operand[1][:, i * P : (i + 1) * P]

        def whole(operand):
            return operand[0][:], operand[1][:]

        def quantise(grouped, width, tag, bufs):
            codes = sb.tile([P, width], U32, tag=tag + "_codes", bufs=bufs, align_bytes=64)
            scales = sb.tile([P, width], U8, tag=tag + "_scales", bufs=bufs, align_bytes=64)
            nc.vector.quantize_mx(out=codes[:].bitcast(FP8X4), scales=scales[:], in_=grouped)
            return codes, scales

        def regroup(grouped, planes):
            nc.vector.tensor_copy(
                out=grouped[:].rearrange("p (c i) t -> p c t i", i=RUN),
                in_=planes[:].rearrange("p t (c i) -> p c t i", i=RUN),
            )

        def gpsimd_regroup(grouped, planes):
            nc.gpsimd.tensor_scalar(
                out=grouped[:], in0=planes[:].rearrange("p t n -> p n t"),
                scalar1=1.0, scalar2=0.0, op0=ALU.mult, op1=ALU.add,
            )

        ident_f32 = sb.tile([P, P], F32)
        make_identity(nc, ident_f32[:])
        ident_bf16 = sb.tile([P, P], BF16)
        make_identity(nc, ident_bf16[:])
        neg_half = sb.tile([P, J], F32)
        nc.vector.memset(neg_half[:], -0.5)
        table_warmer = sb.tile([P, 1], F32)
        floor = sb.tile([P, 1], F32)
        nc.vector.memset(floor[:], FLOOR)

        def load_weight(w_view, split):
            raw = sb.tile([P, PACK, C], BF16, tag="w_raw", bufs=2)
            nc.sync.dma_start(out=raw[:].rearrange(split, u=2), in_=w_view)
            return raw

        def load_first_stage_weight(w):
            return load_weight(
                w.rearrange("(u p e) c -> p u (e c)", u=2, p=P, e=2), "p (u e) c -> p u (e c)"
            )

        def load_second_stage_weight(w):
            return load_weight(
                w.rearrange("(u e p) c -> p u e c", u=2, e=2, p=P), "p (u e) c -> p u e c"
            )

        def group_weight(raw, copy):
            grouped = sb.tile([P, C, PACK], BF16, tag="w_grouped", bufs=2, align_bytes=64)
            copy(grouped, raw)
            return grouped

        def quantise_weight(grouped, name):
            return quantise(grouped[:].rearrange("p c t -> p (c t)"), C, name, 1)

        edge_v = edge.rearrange("(g p j) c -> g p j c", g=N_GROUPS, p=P)
        hk_v = h_k.rearrange("(g p j) t c -> g p j t c", g=N_GROUPS, p=P)
        hm_v = h_m.rearrange("(g p j) t c -> g p j t c", g=N_GROUPS, p=P)
        out_v = out.rearrange("(g p j) c -> g p j c", g=N_GROUPS, p=P)

        edge_rows, edge_grouped, edge_q, q_banks, q_t = {}, {}, {}, {}, {}
        hk_rows, hk_grouped, hk_q, k_banks = {}, {}, {}, {}
        hm_rows, hm_grouped, hm_q, msg_banks = {}, {}, {}, {}
        alpha_t, alpha_banks, normed, gate_t = {}, {}, {}, {}
        mean_var, rstd, shift, last = {}, {}, {}, {}
        gated_t, gated_grouped, gated_q = {}, {}, {}
        v_rows, v_stats, softplus, u_banks = {}, {}, {}, {}

        def load_rows(view, tag, bufs):
            rows = sb.tile([P, J, C], BF16, tag=tag, bufs=bufs)
            nc.sync.dma_start(out=rows[:], in_=view)
            return rows

        def is_step(s):
            return 0 <= s < N_STEPS

        def starts_group(s):
            return is_step(s) and s % T == 0

        def load_step(s):
            if starts_group(s + 1):
                edge_rows[(s + 1) // T] = load_rows(edge_v[(s + 1) // T], "edge_rows", N_GROUPS)
            if is_step(s):
                g, t = divmod(s, T)
                hk_rows[s] = load_rows(hk_v[g][:, :, t, :], "hk_rows", LOAD_AHEAD)
                hm_rows[s] = load_rows(hm_v[g][:, :, t, :], "hm_rows", LOAD_AHEAD)

        def transpose_rows(rows):
            grouped = sb.tile([P, PACK * GROUP], BF16, tag="x_grouped", bufs=4, align_bytes=64)
            grouped_words = grouped[:].bitcast(F32).rearrange("p (n u) -> p n u", u=2)
            for half in range(2):
                bank = psum.tile([P, 2, 2 * P], F32, tag="bank")
                for jj in range(2):
                    words = rows[:, 2 * half + jj, :].bitcast(F32)
                    for u in range(2):
                        nc.tensor.transpose(
                            bank[:, u, jj * P : (jj + 1) * P],
                            words[:, u * P : (u + 1) * P],
                            ident_f32[:],
                        )
                nc.scalar.copy(
                    out=grouped_words[:, half * 2 * P : (half + 1) * 2 * P, :],
                    in_=bank[:].rearrange("p u n -> p n u"),
                )
            return grouped

        def transpose_edge(s):
            if starts_group(s + 1):
                edge_grouped[(s + 1) // T] = transpose_rows(edge_rows[(s + 1) // T])

        def transpose_hk(s):
            if is_step(s):
                hk_grouped[s] = transpose_rows(hk_rows[s])

        def transpose_hm(s):
            if is_step(s):
                hm_grouped[s] = transpose_rows(hm_rows[s])

        def quantise_edge(s):
            if starts_group(s + 1):
                edge_q[(s + 1) // T] = quantise(edge_grouped[(s + 1) // T][:], GROUP, "edge", 2)

        def quantise_hk(s):
            if is_step(s):
                hk_q[s] = quantise(hk_grouped[s][:], GROUP, "hk", 2)

        def quantise_hm(s):
            if is_step(s):
                hm_q[s] = quantise(hm_grouped[s][:], GROUP, "hm", 3)

        def product(banks, key, weight, moving, cts):
            for ct in cts:
                banks[key, ct] = psum.tile([P, GROUP], F32, tag="bank", name="acc")
                matmul_mx(banks[key, ct][:], columns(weight, ct), whole(moving))

        def q_project(g):
            product(q_banks, g, wq, edge_q[g], ALL)
            q_t[g] = sb.tile([P, CT, GROUP], F32, tag="q_t", bufs=2, name="q_t")
            for ct in ALL:
                nc.scalar.activation(
                    out=q_t[g][:, ct, :], in_=q_banks[g, ct][:], func=ACT.Identity,
                    bias=bq_scaled_col[:, ct : ct + 1], scale=inv_sqrt_c,
                )

        def k_project(s, cts):
            if is_step(s):
                product(k_banks, s, wk, hk_q[s], cts)

        def alpha(s, cts):
            if not is_step(s):
                return
            if 0 in cts:
                alpha_t[s] = sb.tile([P, CT, GROUP], F32, tag="alpha_t", bufs=2, name="alpha_t")
            for ct in cts:
                nc.vector.scalar_tensor_tensor(
                    out=alpha_t[s][:, ct, :], in0=k_banks[s, ct][:], scalar=bk2_col[:, ct : ct + 1],
                    in1=q_t[s // T][:, ct, :], op0=ALU.add, op1=ALU.mult,
                )

        def alpha_rows(s, j):
            bank = psum.tile([P, C], F32, tag="bank", name="alpha_bank")
            for ct in range(CT):
                nc.tensor.transpose(
                    bank[:, ct * P : (ct + 1) * P],
                    alpha_t[s][:, ct, j * P : (j + 1) * P],
                    ident_f32[:],
                )
            alpha_banks[s, j] = bank
            return bank

        def statistics(s, tiles):
            if is_step(s):
                for j in tiles:
                    bank = alpha_rows(s, j)
                    nc.vector.bn_stats(out=bn_triples[s % 2][:, j, 0:6], in_=bank[:])

        def aggregate(s, tiles):
            if not is_step(s):
                return
            if 0 in tiles:
                mean_var[s] = sb.tile([P, J, 2], F32, tag="alpha_mean_var", bufs=2, name="mean_var")
                rstd[s] = sb.tile([P, J], F32, tag="alpha_rstd", bufs=2, name="rstd")
                shift[s] = sb.tile([P, J], F32, tag="alpha_shift", bufs=2, name="shift")
            for j in tiles:
                nc.vector.bn_aggr(out=mean_var[s][:, j, :], in_=bn_triples[s % 2][:, j, :])

        def power(s, tiles):
            if is_step(s):
                a, b = tiles[0], tiles[-1] + 1
                nc.gpsimd.tensor_tensor(
                    out=rstd[s][:, a:b], in0=mean_var[s][:, a:b, 1], in1=neg_half[:, a:b], op=ALU.pow
                )

        def shift_of(s, tiles):
            if is_step(s):
                a, b = tiles[0], tiles[-1] + 1
                nc.vector.scalar_tensor_tensor(
                    out=shift[s][:, a:b], in0=mean_var[s][:, a:b, 0], scalar=-1.0, in1=rstd[s][:, a:b],
                    op0=ALU.mult, op1=ALU.mult,
                )

        def last_mean(s):
            if not is_step(s):
                return
            bank = alpha_rows(s, 3)
            last[s] = tuple(
                sb.tile([P, 1], F32, tag="last_" + tag, bufs=2, name=tag)
                for tag in ("neg_mean", "deviation", "var_eps", "rstd", "shift")
            )
            neg_mean = last[s][0]
            unused = sb.tile([P, C], BF16, tag="unused", bufs=1)
            nc.scalar.activation(
                out=unused[:], in_=bank[:], func=ACT.Identity, scale=-1.0 / C, accum_out=neg_mean[:]
            )

        def last_deviation(s):
            if is_step(s):
                neg_mean, deviation = last[s][0:2]
                unused = sb.tile([P, C], BF16, tag="unused", bufs=1)
                nc.scalar.activation(
                    out=unused[:], in_=alpha_banks[s, 3][:], func=ACT.Square, bias=neg_mean[:],
                    accum_out=deviation[:],
                )

        def last_power(s):
            if is_step(s):
                neg_mean, deviation, var_eps, last_rstd, last_shift = last[s]
                nc.gpsimd.tensor_scalar(
                    out=var_eps[:], in0=deviation[:], scalar1=1.0 / C, scalar2=EPS,
                    op0=ALU.mult, op1=ALU.add,
                )
                nc.gpsimd.tensor_tensor(out=last_rstd[:], in0=var_eps[:], in1=neg_half[:, 0:1], op=ALU.pow)
                nc.gpsimd.tensor_tensor(out=last_shift[:], in0=neg_mean[:], in1=last_rstd[:], op=ALU.mult)

        def normalise(s, tiles):
            if not is_step(s):
                return
            if 0 in tiles:
                normed[s] = sb.tile([P, J, C], F32, tag="normed", bufs=1, name="normed")
            for j in tiles:
                scale, bias = rstd[s][:, j : j + 1], shift[s][:, j : j + 1]
                if j == 3:
                    scale, bias = last[s][3][:], last[s][4][:]
                nc.scalar.activation(
                    out=normed[s][:, j, :], in_=alpha_banks[s, j][:], func=ACT.Identity,
                    bias=bias, scale=scale,
                )

        def sigmoid(s, cts):
            if not is_step(s):
                return
            if 0 in cts:
                gate_t[s] = sb.tile([P, CT, GROUP], F32, tag="gate_t", bufs=1, name="gate_t")
            for ct in cts:
                bank = psum.tile([P, GROUP], F32, tag="bank")
                for j in range(J):
                    nc.tensor.transpose(
                        bank[:, j * P : (j + 1) * P],
                        normed[s][:, j, ct * P : (ct + 1) * P],
                        ident_f32[:],
                    )
                nc.scalar.activation(
                    out=gate_t[s][:, ct, :], in_=bank[:], func=ACT.Sigmoid,
                    bias=b_att_col[:, ct : ct + 1], scale=g_att_col[:, ct : ct + 1],
                )

        def msg_project(s, cts):
            if is_step(s):
                product(msg_banks, s, wm, hm_q[s], cts)

        def gate_multiply(s, cts):
            if not is_step(s):
                return
            if 0 in cts:
                gated_t[s] = sb.tile([P, CT, GROUP], BF16, tag="gated_t", bufs=2, name="gated_t")
            for ct in cts:
                nc.vector.scalar_tensor_tensor(
                    out=gated_t[s][:, ct, :], in0=msg_banks[s, ct][:], scalar=bm2_col[:, ct : ct + 1],
                    in1=gate_t[s][:, ct, :], op0=ALU.add, op1=ALU.mult,
                )

        def gate_regroup(s, copy):
            if not is_step(s):
                return
            gated_grouped[s] = sb.tile(
                [P, GROUP, PACK], BF16, tag="gated_grouped", bufs=2, align_bytes=64, name="gated_grouped"
            )
            copy(gated_grouped[s], gated_t[s])

        def gate_quantise(s):
            if is_step(s):
                gated_q[s] = quantise(gated_grouped[s][:].rearrange("p n t -> p (n t)"), GROUP, "gated", T + 1)

        def u_product(g, j, directions):
            if 0 in directions:
                u_banks[g, j] = psum.tile([P, C], F32, tag="bank", name="u_bank")
            for t in directions:
                matmul_mx(
                    u_banks[g, j][:], columns(gated_q[T * g + t], j), whole(wc),
                    start=(t == 0), stop=(t == T - 1),
                )

        def u_statistics(g, j):
            if j == 0:
                v_rows[g] = sb.tile([P, J, C], F32, tag="v_rows", bufs=N_GROUPS, name="v_rows")
                softplus[g] = sb.tile([P, J, C], F32, tag="softplus", bufs=N_GROUPS, name="softplus")
                v_stats[g] = tuple(
                    sb.tile([P, J], F32, tag="u_" + tag, bufs=2, name=tag)
                    for tag in ("mean", "deviation", "v_mean", "var_eps", "rstd")
                )
            v = v_rows[g]
            mean, deviation, v_mean, var_eps, v_rstd = v_stats[g]
            nc.vector.scalar_tensor_tensor(
                out=v[:, j, :], in0=u_banks[g, j][:], scalar=1.0 / C, in1=bc_sum[:],
                op0=ALU.mult, op1=ALU.add, accum_out=mean[:, j : j + 1],
            )
            nc.scalar.activation(
                out=softplus[g][:, j, :], in_=v[:, j, :], func=ACT.Square,
                scale=-float(C), bias=mean[:, j : j + 1], accum_out=deviation[:, j : j + 1],
            )

        def u_rstd(g, tiles):
            mean, deviation, v_mean, var_eps, v_rstd = v_stats[g]
            a, b = tiles[0], tiles[-1] + 1
            nc.gpsimd.tensor_scalar(
                out=v_mean[:, a:b], in0=mean[:, a:b], scalar1=1.0 / C, scalar2=0.0, op0=ALU.mult, op1=ALU.add
            )
            nc.gpsimd.tensor_scalar(
                out=var_eps[:, a:b], in0=deviation[:, a:b], scalar1=C ** -3.0, scalar2=EPS * C ** -2.0,
                op0=ALU.mult, op1=ALU.add,
            )
            nc.gpsimd.tensor_tensor(out=v_rstd[:, a:b], in0=var_eps[:, a:b], in1=neg_half[:, a:b], op=ALU.pow)

        def edge_plus_b_bn(g, j):
            bank = psum.tile([P, C], F32, tag="bank", name="residual")
            nc.tensor.matmul(bank[:], ident_bf16[:], edge_rows[g][:, j, :], start=True, stop=False)
            nc.tensor.matmul(bank[:], ident_bf16[:], b_bn_bc[:], start=False, stop=True)
            return bank

        def scale_deviation(g, tiles):
            v, v_mean = v_rows[g], v_stats[g][2]
            for j in tiles:
                nc.vector.scalar_tensor_tensor(
                    out=v[:, j, :], in0=v[:, j, :], scalar=v_mean[:, j : j + 1], in1=g_bn_bc[:],
                    op0=ALU.subtract, op1=ALU.mult,
                )

        def add_edge(g, tiles):
            v, v_rstd = v_rows[g], v_stats[g][4]
            for j in tiles:
                residual = edge_plus_b_bn(g, j)
                nc.vector.scalar_tensor_tensor(
                    out=v[:, j, :], in0=v[:, j, :], scalar=v_rstd[:, j : j + 1], in1=residual[:],
                    op0=ALU.mult, op1=ALU.add,
                )

        def sigmoid_of_minus(g, tiles):
            for j in tiles:
                nc.scalar.activation(
                    out=softplus[g][:, j, :], in_=v_rows[g][:, j, :], func=ACT.Sigmoid, scale=-1.0
                )

        def logarithm(g, tiles):
            for j in tiles:
                nc.scalar.activation(
                    out=softplus[g][:, j, :], in_=softplus[g][:, j, :], func=ACT.Ln, bias=floor[:]
                )

        def load_sigmoid_table():
            nc.scalar.activation(out=table_warmer[:], in_=neg_half[:, 0:1], func=ACT.Sigmoid)

        def store(g, tiles):
            for j in tiles:
                nc.vector.scalar_tensor_tensor(
                    out=softplus[g][:, j, :], in0=softplus[g][:, j, :], scalar=-1.0,
                    in1=v_rows[g][:, j, :], op0=ALU.mult, op1=ALU.max,
                )
                nc.sync.dma_start(out=out_v[g][:, j, :], in_=softplus[g][:, j, :])

        ALL, LOW, HIGH = range(J), (0, 1), (2, 3)
        bn_triples = []
        for x in range(2):
            triples = sb.tile([P, J, 9], F32, name="bn_triples%d" % x)
            nc.vector.memset(triples[:], 0.0)
            nc.vector.tensor_scalar_add(out=triples[:, :, 8], in0=triples[:, :, 7], scalar1=C * EPS)
            bn_triples.append(triples)
        load_sigmoid_table()
        load_step(-1)
        wq_raw = load_first_stage_weight(Wq)
        vec_rows = sb.tile([P, P], BF16)
        nc.vector.memset(vec_rows[:], 0.0)
        for v, vec in enumerate((bq, bk2, bm2, g_att, b_att)):
            nc.sync.dma_start(
                out=vec_rows[v * CT : (v + 1) * CT, :], in_=vec.rearrange("(t p) -> t p", p=P)
            )
        hk_rows[0] = load_rows(hk_v[0][:, :, 0, :], "hk_rows", LOAD_AHEAD)
        wk_raw = load_first_stage_weight(Wk2)
        hm_rows[0] = load_rows(hm_v[0][:, :, 0, :], "hm_rows", LOAD_AHEAD)
        transpose_edge(-1)
        cols_ps = psum.tile([P, P], BF16, tag="bank")
        nc.tensor.transpose(cols_ps[:], vec_rows[:], ident_bf16[:])
        cols = sb.tile([P, P], F32)
        nc.vector.tensor_copy(out=cols[:], in_=cols_ps[:])
        bk2_col = cols[:, 1 * CT : 2 * CT]
        bm2_col = cols[:, 2 * CT : 3 * CT]
        g_att_col = cols[:, 3 * CT : 4 * CT]
        b_att_col = cols[:, 4 * CT : 5 * CT]
        inv_sqrt_c = 1.0 / math.sqrt(C)
        bq_scaled_col = sb.tile([P, CT], F32)
        nc.vector.tensor_scalar_mul(out=bq_scaled_col[:], in0=cols[:, 0:CT], scalar1=inv_sqrt_c)

        wq_grouped = group_weight(wq_raw, regroup)
        quantise_edge(-1)
        wq = quantise_weight(wq_grouped, "wq")
        transpose_hk(0)
        q_project(0)
        wk_grouped = group_weight(wk_raw, regroup)
        quantise_hk(0)
        wk = quantise_weight(wk_grouped, "wk")
        k_project(0, ALL)
        load_step(1)
        wm_raw = load_first_stage_weight(Wm2)
        wc_raw = load_second_stage_weight(Wc)
        load_step(2)
        bc_bc = sb.tile([P, C], BF16)
        nc.sync.dma_start(out=bc_bc[:], in_=bc.partition_broadcast(P))
        g_bn_bc = sb.tile([P, C], BF16)
        nc.sync.dma_start(out=g_bn_bc[:], in_=g_bn.partition_broadcast(P))
        b_bn_bc = sb.tile([P, C], BF16)
        nc.sync.dma_start(out=b_bn_bc[:], in_=b_bn.partition_broadcast(P))
        transpose_hk(1)
        alpha(0, ALL)

        for i in range(N_STEPS):
            gated = i - 1
            ended, age = divmod(i - (T + 1), T)
            statistics(i, LOW)
            sigmoid(gated, LOW)
            quantise_hk(i + 1)
            aggregate(i, LOW)
            gate_quantise(gated - 1)
            quantise_edge(i + 1)
            if i == 1:
                wm = quantise_weight(wm_grouped, "wm")
                wc_grouped = group_weight(wc_raw, regroup)
            if i == 2:
                wc = quantise_weight(wc_grouped, "wc")
                bc_sum = sb.tile([P, C], F32)
                nc.vector.tensor_scalar_mul(out=bc_sum[:], in0=bc_bc[:], scalar1=float(T) / C)
            if ended >= 0 and age == 1:
                scale_deviation(ended, LOW)
            if ended >= 0 and age == 2:
                scale_deviation(ended, HIGH)
            power(i, LOW)
            if starts_group(i + 1):
                q_project((i + 1) // T)
            msg_project(gated, LOW)
            gate_multiply(gated, LOW)
            statistics(i, (2,))
            last_mean(i)
            if i == 0:
                transpose_hm(0)
            shift_of(i, LOW)
            aggregate(i, (2,))
            sigmoid(gated, HIGH)
            last_deviation(i)
            quantise_hm(i)
            msg_project(gated, HIGH)
            power(i, (2,))
            last_power(i)
            gate_multiply(gated, HIGH)
            shift_of(i, (2,))
            k_project(i + 1, LOW)
            k_project(i + 1, HIGH)
            normalise(i, LOW)
            if i == 0:
                transpose_edge(i + TRANSPOSE_AHEAD)
            gate_regroup(gated, gpsimd_regroup if i < N_STEPS - 1 else regroup)
            alpha(i + 1, LOW)
            transpose_hk(i + TRANSPOSE_AHEAD)
            normalise(i, HIGH)
            alpha(i + 1, HIGH)
            if i == 0:
                wm_grouped = group_weight(wm_raw, regroup)
            transpose_hm(i + 1)
            if i > 0:
                transpose_edge(i + TRANSPOSE_AHEAD)
            load_step(i + LOAD_AHEAD)
            if ended >= 0 and age == 0:
                for j in ALL:
                    u_product(ended, j, range(T))
                    u_statistics(ended, j)
                u_rstd(ended, ALL)
            if ended >= 0 and age == 1:
                add_edge(ended, LOW)
                sigmoid_of_minus(ended, LOW)
            if ended >= 0 and age == 2:
                add_edge(ended, HIGH)
                sigmoid_of_minus(ended, HIGH)

        s, g = N_STEPS - 1, N_GROUPS - 1
        gate_quantise(s - 1)
        scale_deviation(g - 1, HIGH)
        msg_project(s, ALL)
        sigmoid(s, ALL)
        gate_multiply(s, ALL)
        gate_regroup(s, regroup)
        gate_quantise(s)
        logarithm(0, ALL)
        for j in ALL:
            u_product(g, j, range(T - 1))
        for j in ALL:
            u_product(g, j, [T - 1])
            u_statistics(g, j)
            if j == 1:
                u_rstd(g, LOW)
        load_sigmoid_table()
        u_rstd(g, HIGH)
        add_edge(g - 1, HIGH)
        sigmoid_of_minus(g - 1, HIGH)
        scale_deviation(g, LOW)
        add_edge(g, LOW)
        scale_deviation(g, HIGH)
        add_edge(g, HIGH)
        sigmoid_of_minus(g, ALL)
        store(0, ALL)
        logarithm(1, ALL)
        store(1, ALL)
        logarithm(g, ALL)
        store(g, ALL)
